import numpy as np
import ml_dtypes


def mxq(x, axis, fmt="e4m3"):
    dtype, down = {"e4m3": (ml_dtypes.float8_e4m3fn, 7), "e5m2": (ml_dtypes.float8_e5m2, 14)}[fmt]
    v = np.moveaxis(np.asarray(x, np.float32).astype(ml_dtypes.bfloat16).astype(np.float64), axis, -1)
    blocks = v.reshape(v.shape[:-1] + (-1, 32))
    amax = np.abs(blocks).max(-1, keepdims=True)
    byte = np.maximum(np.where(amax > 0, np.frexp(amax)[1] - 1 + 127, 0) - down, 1)
    scale = np.exp2(byte - 127.0)
    codes = (blocks / scale).astype(np.float32).astype(dtype).astype(np.float64)
    return np.moveaxis((codes * scale).reshape(v.shape), -1, axis)


WIDE = False


def mx_kscale(k):
    if not WIDE:
        return np.ones(k)
    levels = np.array([10, -10, 5, -5, 0])
    if k % 512:
        return np.exp2(np.random.permutation(np.resize(levels, k // 32))).repeat(32)
    a = np.empty((k // 512, 16))
    for p in range(k // 512):
        a[p, :8] = np.random.permutation(np.resize(levels, 8))
        for g in range(8):
            far = levels[np.abs(levels - a[p, g]) >= 10]
            a[p, g + 8] = far[np.random.randint(len(far))]
    return np.exp2(a.ravel()).repeat(32)


BF16 = ml_dtypes.bfloat16


def bf(x):
    return np.asarray(x, np.float32).astype(BF16)


def f64(x):
    return np.asarray(x).astype(np.float64)


B, T, D, H, HKV, HD, R, DFF = 2, 2048, 512, 4, 2, 128, 128, 6144
HALF = HD // 2
EPS = 1e-6
THETA = 1e6


def rms_norm(x, w):
    return x / np.sqrt(np.mean(x * x, axis=-1, keepdims=True) + EPS) * w


def rotate_half(x):
    return np.concatenate([-x[..., HALF:], x[..., :HALF]], axis=-1)


def setup_inputs():
    rn = np.random.standard_normal
    s = mx_kscale(D)
    inv_freq = 1.0 / THETA ** (np.arange(HALF) / HALF)
    freqs = np.arange(T)[:, None] * inv_freq[None, :]
    emb = np.concatenate([freqs, freqs], axis=-1)
    return {
        "hidden_states": bf(rn((B, T, D)) * np.exp(0.5 * rn((B, T, 1)))),
        "ln1_w": bf((1.0 + 0.1 * rn(D)) * s),
        "Wq": bf(rn((D, H * HD)) / np.sqrt(D) / s[:, None]),
        "Wk": bf(rn((D, HKV * HD)) / np.sqrt(D) / s[:, None]),
        "Wv": bf(rn((D, HKV * HD)) / np.sqrt(D) / s[:, None]),
        "q_norm_w": bf(1.0 + 0.1 * rn(HD)),
        "k_norm_w": bf(1.0 + 0.1 * rn(HD)),
        "cos": bf(np.cos(emb)),
        "sin": bf(np.sin(emb)),
    }


def reference(hidden_states, ln1_w, Wq, Wk, Wv, q_norm_w, k_norm_w, cos, sin):
    h = rms_norm(f64(hidden_states), f64(ln1_w))
    hq = mxq(h, 2, "e4m3")
    q = rms_norm((hq @ mxq(f64(Wq), 0, "e4m3")).reshape(B, T, H, HD), f64(q_norm_w)).transpose(0, 2, 1, 3)
    k = rms_norm((hq @ mxq(f64(Wk), 0, "e4m3")).reshape(B, T, HKV, HD), f64(k_norm_w)).transpose(0, 2, 1, 3)
    v = (hq @ mxq(f64(Wv), 0, "e4m3")).reshape(B, T, HKV, HD).transpose(0, 2, 1, 3)
    c, s_ = f64(cos)[None, None], f64(sin)[None, None]
    q = q * c + rotate_half(q) * s_
    k = k * c + rotate_half(k) * s_
    return q, k, v

@@ -1,0 +1,304 @@
+from contextlib import ExitStack
+
+import concourse.mybir as mybir
+from concourse.masks import make_identity
+
+F32 = mybir.dt.float32
+BF16 = mybir.dt.bfloat16
+U32 = mybir.dt.uint32
+U8 = mybir.dt.uint8
+FP8X4 = mybir.dt.float8_e4m3fn_x4
+ALU = mybir.AluOpType
+ACT = mybir.ActivationFunctionType
+
+P = 128
+B, T, D = 2, 2048, 512
+HD = 128
+HALF = 64
+NQ, NK, NV = 4, 2, 2
+NOUT = (NQ + NK + NV) * HD
+TPP = T // P
+GRP = 4
+EPS = 1e-6
+FLOPS = 2 * B * T * D * NOUT
+
+
+def tile_rawkvinjector_pa_t_kernel(
+    tc, hidden_states, ln1_w, Wq, Wk, Wv, q_norm_w, k_norm_w, cos, sin, out_0, out_1, out_2
+):
+    nc = tc.nc
+    n_tiles = B * TPP
+    n_pairs = n_tiles // 2
+    BATCHES = ((0,), (1,)) + tuple((pr, pr + 1) for pr in range(2, n_pairs, 2))
+    BATCH_OF = dict((pr, bt) for bt, prs in enumerate(BATCHES) for pr in prs)
+    with ExitStack() as ctx:
+        const = ctx.enter_context(tc.tile_pool(name="const", bufs=1))
+        small = ctx.enter_context(tc.tile_pool(name="small", bufs=4))
+        junk = ctx.enter_context(tc.tile_pool(name="junk", bufs=4))
+        hpool = ctx.enter_context(tc.tile_pool(name="hpool", bufs=3))
+        codes = ctx.enter_context(tc.tile_pool(name="codes", bufs=4))
+        zpool = ctx.enter_context(tc.tile_pool(name="zpool", bufs=4))
+        obpool = ctx.enter_context(tc.tile_pool(name="obpool", bufs=3))
+        psum_c = ctx.enter_context(tc.psum_pool(name="psum_c", bufs=1))
+        psum_t = ctx.enter_context(tc.psum_pool(name="psum_t", bufs=1))
+        psum_a = ctx.enter_context(tc.psum_pool(name="psum_a", bufs=3))
+        psum_b = ctx.enter_context(tc.psum_pool(name="psum_b", bufs=3))
+        ctx.enter_context(tc.manual_schedule())
+
+        def where(n):
+            grp = n // GRP
+            return grp % B, grp // B, n % GRP
+
+        eps = const.tile([P, 1], F32)
+        nc.vector.memset(eps[:], EPS)
+        warm = const.tile([P, 1], F32)
+        nc.scalar.activation(out=warm[:], in_=eps[:], func=ACT.Abs_reciprocal_sqrt)
+        zrow = const.tile([P, D + 2 * HD], BF16)
+        nc.vector.memset(zrow[:], 0.0)
+        ones = const.tile([P, P], BF16)
+        nc.vector.memset(ones[:], 1.0)
+        ident = const.tile([P, P], BF16)
+        make_identity(nc, ident[:])
+
+        nc.scalar.dma_start(out=zrow[0:1, 0:D], in_=ln1_w.unsqueeze(0))
+        nc.scalar.dma_start(out=zrow[0:1, D : D + HD], in_=q_norm_w.unsqueeze(0))
+        nc.scalar.dma_start(out=zrow[0:1, D + HD : D + 2 * HD], in_=k_norm_w.unsqueeze(0))
+        x_view = [hidden_states[b].rearrange("(p i) k -> p i k", i=TPP) for b in range(B)]
+        x_sb = [const.tile([P, 2, D], BF16, name="x_%d" % pr) for pr in range(n_pairs)]
+
+        def load_x(pr):
+            b, g, ii = where(2 * pr)
+            i = GRP * g + ii
+            nc.sync.dma_start(out=x_sb[pr][:], in_=x_view[b][:, i : i + 2, :])
+
+        load_x(0)
+        load_x(1)
+        load_x(2)
+        wq_raw = const.tile([P, 4, NQ * HD], BF16)
+        wk_raw = const.tile([P, 4, NK * HD], BF16)
+        wv_raw = const.tile([P, 4, NV * HD], BF16)
+        nc.sync.dma_start(out=wq_raw[:], in_=Wq.rearrange("(p t) n -> p t n", t=4))
+        nc.sync.dma_start(out=wk_raw[:], in_=Wk.rearrange("(p t) n -> p t n", t=4))
+        nc.sync.dma_start(out=wv_raw[:], in_=Wv.rearrange("(p t) n -> p t n", t=4))
+        load_x(3)
+        cs_raw = const.tile([P, 2, TPP, HD], BF16)
+        nc.sync.dma_start(out=cs_raw[:, 0, :, :], in_=cos.rearrange("(p i) d -> p i d", i=TPP))
+        sin_view = sin.rearrange("(p i) d -> p i d", i=TPP)
+        nc.sync.dma_start(out=cs_raw[:, 1, :, 0:HALF], in_=sin_view[:, :, HALF:HD])
+        nc.sync.dma_start(out=cs_raw[:, 1, :, HALF:HD], in_=sin_view[:, :, 0:HALF])
+        for pr in range(4, n_pairs):
+            load_x(pr)
+
+        lnw_ps = psum_c.tile([P, 4, P], F32)
+        for t in range(4):
+            nc.tensor.matmul(
+                out=lnw_ps[:, t, :], lhsT=ones[:], rhs=zrow[:, t:D:4], start=True, stop=True
+            )
+        wn_ps = psum_t.tile([P, 2, HD], F32, tag="tp")
+        nc.tensor.matmul(
+            out=wn_ps[:].rearrange("p a d -> p (a d)"), lhsT=ones[:], rhs=zrow[:, D : D + 2 * HD],
+            start=True, stop=True,
+        )
+        wtab = const.tile([P, 2, 2, HD], BF16)
+        tab = const.tile([P, TPP, 2, 2, HD], F32)
+
+        def norm_weight_table():
+            nc.scalar.copy(out=wtab[:, 0, :, :], in_=wn_ps[:])
+            nc.scalar.copy(out=wtab[:, 1, :, 0:HALF], in_=wn_ps[:, :, 0:HALF])
+            nc.scalar.mul(out=wtab[:, 1, :, HALF:HD], in_=wn_ps[:, :, HALF:HD], mul=-1.0)
+
+        def build_table(i):
+            nc.gpsimd.tensor_tensor(
+                out=tab[:, i, :, :, :].rearrange("p q c d -> p c q d"),
+                in0=cs_raw[:, :, i, :].unsqueeze(2).to_broadcast([P, 2, 2, HD]),
+                in1=wtab[:],
+                op=ALU.mult,
+            )
+
+        wg = const.tile([P, NOUT, 4], BF16, align_bytes=64)
+        wc = const.tile([P, NOUT], U32, align_bytes=64)
+        ws = const.tile([P, NOUT], U8, align_bytes=64)
+
+        def weights():
+            for raw, c0, c1 in ((wq_raw, 0, 512), (wk_raw, 512, 768), (wv_raw, 768, 1024)):
+                nc.vector.tensor_copy(
+                    out=wg[:, c0:c1, :].rearrange("p (c i) t -> p c t i", i=4),
+                    in_=raw[:].rearrange("p t (c i) -> p c t i", i=4),
+                )
+            for c in range(2):
+                cols = slice(512 * c, 512 * (c + 1))
+                nc.vector.quantize_mx(
+                    out=wc[:, cols].bitcast(FP8X4),
+                    scales=ws[:, cols],
+                    in_=wg[:, cols, :].rearrange("p n t -> p (n t)"),
+                )
+
+        r0s, hs_, tps, hgs, h_codes, accs, rs, obs = {}, {}, {}, {}, {}, {}, {}, {}
+
+        def stats(pr):
+            ss0 = small.tile([P, 2], F32)
+            for a in range(2):
+                sq = junk.tile([P, D], BF16)
+                nc.scalar.activation(
+                    out=sq[:], in_=x_sb[pr][:, a, :], func=ACT.Square, accum_out=ss0[:, a : a + 1]
+                )
+            r0 = small.tile([P, 2], F32)
+            nc.scalar.activation(
+                out=r0[:], in_=ss0[:], func=ACT.Abs_reciprocal_sqrt, scale=1.0 / D, bias=eps[:, 0:1]
+            )
+            r0s[pr] = r0
+
+        def norm(pr):
+            h = hpool.tile([P, 2, D], BF16)
+            for a in range(2):
+                nc.vector.scalar_tensor_tensor(
+                    out=h[:, a, :].rearrange("p (t c) -> p t c", t=4),
+                    in0=x_sb[pr][:, a, :].rearrange("p (c t) -> p t c", t=4),
+                    scalar=r0s[pr][:, a : a + 1], in1=lnw_ps[:],
+                    op0=ALU.mult, op1=ALU.mult,
+                )
+            hs_[pr] = h
+
+        def transp(pr):
+            tp = psum_t.tile([P, 2, 4, P], BF16, tag="tp")
+            for a in range(2):
+                for t in range(4):
+                    nc.tensor.transpose(
+                        out=tp[:, a, t, :], in_=hs_[pr][:, a, P * t : P * (t + 1)], identity=ident[:]
+                    )
+            tps[pr] = tp
+
+        def evac(pr):
+            bt = BATCH_OF[pr]
+            if pr == BATCHES[bt][0]:
+                hgs[bt] = hpool.tile([P, 2 * len(BATCHES[bt]), P, 4], BF16, align_bytes=64, name="hg", tag="hg")
+            a0 = 2 * (pr - BATCHES[bt][0])
+            nc.scalar.copy(out=hgs[bt][:, a0 : a0 + 2, :, :], in_=tps[pr][:].rearrange("p a t r -> p a r t"))
+
+        def quant(bt):
+            width = 2 * P * len(BATCHES[bt])
+            hc = codes.tile([P, width], U32, align_bytes=64)
+            hs = codes.tile([P, width], U8, align_bytes=64)
+            nc.vector.quantize_mx(
+                out=hc[:].bitcast(FP8X4), scales=hs[:], in_=hgs[bt][:].rearrange("p a r t -> p (a r t)")
+            )
+            h_codes[bt] = (hc, hs)
+
+        def mx(n):
+            bt = BATCH_OF[n // 2]
+            hc, hs = h_codes[bt]
+            first = n - 2 * BATCHES[bt][0]
+            tok = slice(P * first, P * (first + 1))
+            pa = psum_a.tile([P, 512], F32)
+            pb = psum_b.tile([P, 512], F32)
+            for c, acc in enumerate((pa, pb)):
+                cols = slice(512 * c, 512 * (c + 1))
+                nc.tensor.matmul_mx(
+                    out=acc[:],
+                    lhsT=hc[:, tok].bitcast(FP8X4), lhsT_scale=hs[:, tok],
+                    rhs=wc[:, cols].bitcast(FP8X4), rhs_scale=ws[:, cols],
+                    start=True, stop=True,
+                )
+            heads = [pa[:, HD * k : HD * (k + 1)] for k in range(NQ)]
+            heads += [pb[:, HD * k : HD * (k + 1)] for k in range(NK)]
+            accs[n] = (heads, pb)
+
+        def sq_heads(n):
+            b, g, ii = where(n)
+            if ii == 0:
+                obs[n // GRP] = obpool.tile([P, 8, GRP, HD], F32, name="ob")
+            ob = obs[n // GRP]
+            heads, pb = accs[n]
+            ss = small.tile([P, 6], F32)
+            for k, u in enumerate(heads):
+                sq1 = junk.tile([P, HD], BF16)
+                nc.scalar.activation(out=sq1[:], in_=u, func=ACT.Square, accum_out=ss[:, k : k + 1])
+            nc.scalar.copy(
+                out=ob[:, 6:8, ii, :], in_=pb[:, 256:512].rearrange("p (h d) -> p h d", h=2)
+            )
+            r = small.tile([P, 6], F32)
+            nc.scalar.activation(
+                out=r[:], in_=ss[:], func=ACT.Abs_reciprocal_sqrt, scale=1.0 / HD, bias=eps[:, 0:1]
+            )
+            rs[n] = r
+
+        def store(grp, i0, i1):
+            b, g = grp % B, grp // B
+            rows = slice(GRP * g + i0, GRP * g + i1)
+            for dst, h0, h1 in ((out_0, 0, 4), (out_1, 4, 6), (out_2, 6, 8)):
+                nc.sync.dma_start(
+                    out=dst[b].rearrange("h (p i) d -> p h i d", i=TPP)[:, :, rows, :],
+                    in_=obs[grp][:, h0:h1, i0:i1, :],
+                )
+
+        def rope(n):
+            b, g, ii = where(n)
+            i = GRP * g + ii
+            ob = obs[n // GRP]
+            heads, pb = accs[n]
+            r = rs[n]
+            z = zpool.tile([P, 6, 2, HD], F32)
+            for k, u in enumerate(heads):
+                qk = 0 if k < NQ else 1
+                nc.vector.scalar_tensor_tensor(
+                    out=z[:, k, :, :], in0=tab[:, i, qk, :, :], scalar=r[:, k : k + 1],
+                    in1=u.unsqueeze(1).to_broadcast([P, 2, HD]),
+                    op0=ALU.mult, op1=ALU.mult,
+                )
+            adder = nc.vector if n == n_tiles - 1 else nc.gpsimd
+            adder.tensor_tensor(
+                out=ob[:, 0:6, ii, :].rearrange("p k (s d) -> p k s d", s=2),
+                in0=z[:, :, 0, :].rearrange("p k (s d) -> p k s d", s=2),
+                in1=z[:, :, 1, :].rearrange("p k (s d) -> p k s d", s=2)[:, :, ::-1, :],
+                op=ALU.add,
+            )
+            if n // GRP == n_tiles // GRP - 1:
+                store(n // GRP, ii, ii + 1)
+            elif ii == GRP - 1:
+                store(n // GRP, 0, GRP)
+
+        def when(f, idx, limit):
+            if 0 <= idx < limit:
+                f(idx)
+
+        stats(0)
+        norm_weight_table()
+        norm(0)
+        transp(0)
+        stats(1)
+        norm(1)
+        stats(2)
+        weights()
+        evac(0)
+        transp(1)
+        quant(0)
+        mx(0)
+        mx(1)
+        build_table(0)
+        stats(3)
+        evac(1)
+        stats(4)
+        sq_heads(0)
+        build_table(1)
+        norm(2)
+        transp(2)
+        quant(1)
+        build_table(2)
+        evac(2)
+        norm(3)
+        transp(3)
+        build_table(3)
+        for j in range(n_pairs):
+            when(mx, 2 * j + 2, n_tiles)
+            when(sq_heads, 2 * j + 1, n_tiles)
+            when(rope, 2 * j, n_tiles)
+            when(mx, 2 * j + 3, n_tiles)
+            when(evac, j + 3, n_pairs)
+            when(norm, j + 4, n_pairs)
+            when(transp, j + 4, n_pairs)
+            when(sq_heads, 2 * j + 2, n_tiles)
+            when(rope, 2 * j + 1, n_tiles)
+            when(build_table, j + 4, TPP)
+            if j + 3 < n_pairs and j + 3 == BATCHES[BATCH_OF[j + 3]][-1]:
+                quant(BATCH_OF[j + 3])
+            when(stats, j + 5, n_pairs)

@@ -29,11 +29,11 @@ def tile_rawkvinjector_pa_t_kernel(
     nc = tc.nc
     n_tiles = B * TPP
     n_pairs = n_tiles // 2
-    BATCHES = ((0,), (1,)) + tuple((pr, pr + 1) for pr in range(2, n_pairs, 2))
-    BATCH_OF = dict((pr, bt) for bt, prs in enumerate(BATCHES) for pr in prs)
+    MX_LEAD, EVAC_LEAD, NORM_LEAD, STATS_LEAD = 2, 4, 6, 10
+    TABLES_FIRST = 5
     with ExitStack() as ctx:
         const = ctx.enter_context(tc.tile_pool(name="const", bufs=1))
-        small = ctx.enter_context(tc.tile_pool(name="small", bufs=4))
+        small = ctx.enter_context(tc.tile_pool(name="small", bufs=8))
         junk = ctx.enter_context(tc.tile_pool(name="junk", bufs=4))
         hpool = ctx.enter_context(tc.tile_pool(name="hpool", bufs=3))
         codes = ctx.enter_context(tc.tile_pool(name="codes", bufs=4))
@@ -49,20 +49,20 @@ def tile_rawkvinjector_pa_t_kernel(
             grp = n // GRP
             return grp % B, grp // B, n % GRP
 
+        zrow = const.tile([P, D + 2 * HD], BF16)
+        nc.gpsimd.memset(zrow[:].bitcast(U32), 0)
         eps = const.tile([P, 1], F32)
         nc.vector.memset(eps[:], EPS)
-        warm = const.tile([P, 1], F32)
-        nc.scalar.activation(out=warm[:], in_=eps[:], func=ACT.Abs_reciprocal_sqrt)
-        zrow = const.tile([P, D + 2 * HD], BF16)
-        nc.vector.memset(zrow[:], 0.0)
         ones = const.tile([P, P], BF16)
         nc.vector.memset(ones[:], 1.0)
+        warm = const.tile([P, 1], F32)
         ident = const.tile([P, P], BF16)
         make_identity(nc, ident[:])
 
         nc.scalar.dma_start(out=zrow[0:1, 0:D], in_=ln1_w.unsqueeze(0))
         nc.scalar.dma_start(out=zrow[0:1, D : D + HD], in_=q_norm_w.unsqueeze(0))
         nc.scalar.dma_start(out=zrow[0:1, D + HD : D + 2 * HD], in_=k_norm_w.unsqueeze(0))
+        nc.scalar.activation(out=warm[:], in_=eps[:], func=ACT.Abs_reciprocal_sqrt)
         x_view = [hidden_states[b].rearrange("(p i) k -> p i k", i=TPP) for b in range(B)]
         x_sb = [const.tile([P, 2, D], BF16, name="x_%d" % pr) for pr in range(n_pairs)]
 
@@ -71,34 +71,41 @@ def tile_rawkvinjector_pa_t_kernel(
             i = GRP * g + ii
             nc.sync.dma_start(out=x_sb[pr][:], in_=x_view[b][:, i : i + 2, :])
 
-        load_x(0)
-        load_x(1)
-        load_x(2)
         wq_raw = const.tile([P, 4, NQ * HD], BF16)
         wk_raw = const.tile([P, 4, NK * HD], BF16)
         wv_raw = const.tile([P, 4, NV * HD], BF16)
+        cs_raw = const.tile([P, 2, TPP, HD], BF16)
+        cos_view = cos.rearrange("(p i) d -> p i d", i=TPP)
+        sin_view = sin.rearrange("(p i) d -> p i d", i=TPP)
+
+        def load_cs(g):
+            rows = slice(GRP * g, GRP * (g + 1))
+            nc.sync.dma_start(out=cs_raw[:, 0, rows, :], in_=cos_view[:, rows, :])
+            nc.sync.dma_start(out=cs_raw[:, 1, rows, 0:HALF], in_=sin_view[:, rows, HALF:HD])
+            nc.sync.dma_start(out=cs_raw[:, 1, rows, HALF:HD], in_=sin_view[:, rows, 0:HALF])
+
         nc.sync.dma_start(out=wq_raw[:], in_=Wq.rearrange("(p t) n -> p t n", t=4))
+        load_x(0)
         nc.sync.dma_start(out=wk_raw[:], in_=Wk.rearrange("(p t) n -> p t n", t=4))
         nc.sync.dma_start(out=wv_raw[:], in_=Wv.rearrange("(p t) n -> p t n", t=4))
-        load_x(3)
-        cs_raw = const.tile([P, 2, TPP, HD], BF16)
-        nc.sync.dma_start(out=cs_raw[:, 0, :, :], in_=cos.rearrange("(p i) d -> p i d", i=TPP))
-        sin_view = sin.rearrange("(p i) d -> p i d", i=TPP)
-        nc.sync.dma_start(out=cs_raw[:, 1, :, 0:HALF], in_=sin_view[:, :, HALF:HD])
-        nc.sync.dma_start(out=cs_raw[:, 1, :, HALF:HD], in_=sin_view[:, :, 0:HALF])
-        for pr in range(4, n_pairs):
+        load_x(1)
+        for g in range(TPP // GRP):
+            load_cs(g)
+            load_x(2 * g + 2)
+            load_x(2 * g + 3)
+        for pr in range(2 * (TPP // GRP) + 2, n_pairs):
             load_x(pr)
 
-        lnw_ps = psum_c.tile([P, 4, P], F32)
-        for t in range(4):
-            nc.tensor.matmul(
-                out=lnw_ps[:, t, :], lhsT=ones[:], rhs=zrow[:, t:D:4], start=True, stop=True
-            )
         wn_ps = psum_t.tile([P, 2, HD], F32, tag="tp")
         nc.tensor.matmul(
             out=wn_ps[:].rearrange("p a d -> p (a d)"), lhsT=ones[:], rhs=zrow[:, D : D + 2 * HD],
             start=True, stop=True,
         )
+        lnw_ps = psum_c.tile([P, 4, P], F32)
+        for t in range(4):
+            nc.tensor.matmul(
+                out=lnw_ps[:, t, :], lhsT=ones[:], rhs=zrow[:, t:D:4], start=True, stop=True
+            )
         wtab = const.tile([P, 2, 2, HD], BF16)
         tab = const.tile([P, TPP, 2, 2, HD], F32)
 
@@ -119,45 +126,53 @@ def tile_rawkvinjector_pa_t_kernel(
         wc = const.tile([P, NOUT], U32, align_bytes=64)
         ws = const.tile([P, NOUT], U8, align_bytes=64)
 
-        def weights():
-            for raw, c0, c1 in ((wq_raw, 0, 512), (wk_raw, 512, 768), (wv_raw, 768, 1024)):
-                nc.vector.tensor_copy(
-                    out=wg[:, c0:c1, :].rearrange("p (c i) t -> p c t i", i=4),
-                    in_=raw[:].rearrange("p t (c i) -> p c t i", i=4),
-                )
-            for c in range(2):
-                cols = slice(512 * c, 512 * (c + 1))
-                nc.vector.quantize_mx(
-                    out=wc[:, cols].bitcast(FP8X4),
-                    scales=ws[:, cols],
-                    in_=wg[:, cols, :].rearrange("p n t -> p (n t)"),
-                )
+        def spread_q():
+            interleave(wq_raw, 0, 512)
+
+        def spread_kv():
+            interleave(wk_raw, 512, 768)
+            interleave(wv_raw, 768, 1024)
+
+        def interleave(raw, c0, c1):
+            nc.vector.tensor_copy(
+                out=wg[:, c0:c1, :].rearrange("p (c i) t -> p c t i", i=4),
+                in_=raw[:].rearrange("p t (c i) -> p c t i", i=4),
+            )
+
+        def quant_w(c):
+            cols = slice(512 * c, 512 * (c + 1))
+            nc.vector.quantize_mx(
+                out=wc[:, cols].bitcast(FP8X4),
+                scales=ws[:, cols],
+                in_=wg[:, cols, :].rearrange("p n t -> p (n t)"),
+            )
 
         r0s, hs_, tps, hgs, h_codes, accs, rs, obs = {}, {}, {}, {}, {}, {}, {}, {}
 
-        def stats(pr):
-            ss0 = small.tile([P, 2], F32)
-            for a in range(2):
-                sq = junk.tile([P, D], BF16)
-                nc.scalar.activation(
-                    out=sq[:], in_=x_sb[pr][:, a, :], func=ACT.Square, accum_out=ss0[:, a : a + 1]
-                )
-            r0 = small.tile([P, 2], F32)
+        def stats(n):
+            pr, a = n // 2, n % 2
+            if a == 0:
+                r0s[pr] = small.tile([P, 2], F32, name="ss0"), small.tile([P, 2], F32, name="r0")
+            ss0, r0 = r0s[pr]
+            sq = junk.tile([P, D], BF16)
             nc.scalar.activation(
-                out=r0[:], in_=ss0[:], func=ACT.Abs_reciprocal_sqrt, scale=1.0 / D, bias=eps[:, 0:1]
+                out=sq[:], in_=x_sb[pr][:, a, :], func=ACT.Square, accum_out=ss0[:, a : a + 1]
             )
-            r0s[pr] = r0
-
-        def norm(pr):
-            h = hpool.tile([P, 2, D], BF16)
-            for a in range(2):
-                nc.vector.scalar_tensor_tensor(
-                    out=h[:, a, :].rearrange("p (t c) -> p t c", t=4),
-                    in0=x_sb[pr][:, a, :].rearrange("p (c t) -> p t c", t=4),
-                    scalar=r0s[pr][:, a : a + 1], in1=lnw_ps[:],
-                    op0=ALU.mult, op1=ALU.mult,
+            if a == 1:
+                nc.scalar.activation(
+                    out=r0[:], in_=ss0[:], func=ACT.Abs_reciprocal_sqrt, scale=1.0 / D, bias=eps[:, 0:1]
                 )
-            hs_[pr] = h
+
+        def norm(n):
+            pr, a = n // 2, n % 2
+            if a == 0:
+                hs_[pr] = hpool.tile([P, 2, D], BF16, name="h")
+            nc.vector.scalar_tensor_tensor(
+                out=hs_[pr][:, a, :].rearrange("p (t c) -> p t c", t=4),
+                in0=x_sb[pr][:, a, :].rearrange("p (c t) -> p t c", t=4),
+                scalar=r0s[pr][1][:, a : a + 1], in1=lnw_ps[:],
+                op0=ALU.mult, op1=ALU.mult,
+            )
 
         def transp(pr):
             tp = psum_t.tile([P, 2, 4, P], BF16, tag="tp")
@@ -169,26 +184,20 @@ def tile_rawkvinjector_pa_t_kernel(
             tps[pr] = tp
 
         def evac(pr):
-            bt = BATCH_OF[pr]
-            if pr == BATCHES[bt][0]:
-                hgs[bt] = hpool.tile([P, 2 * len(BATCHES[bt]), P, 4], BF16, align_bytes=64, name="hg", tag="hg")
-            a0 = 2 * (pr - BATCHES[bt][0])
-            nc.scalar.copy(out=hgs[bt][:, a0 : a0 + 2, :, :], in_=tps[pr][:].rearrange("p a t r -> p a r t"))
+            hgs[pr] = hpool.tile([P, 2, P, 4], BF16, align_bytes=64, name="hg")
+            nc.scalar.copy(out=hgs[pr][:], in_=tps[pr][:].rearrange("p a t r -> p a r t"))
 
-        def quant(bt):
-            width = 2 * P * len(BATCHES[bt])
-            hc = codes.tile([P, width], U32, align_bytes=64)
-            hs = codes.tile([P, width], U8, align_bytes=64)
+        def quant(pr):
+            hc = codes.tile([P, 2 * P], U32, align_bytes=64)
+            hs = codes.tile([P, 2 * P], U8, align_bytes=64)
             nc.vector.quantize_mx(
-                out=hc[:].bitcast(FP8X4), scales=hs[:], in_=hgs[bt][:].rearrange("p a r t -> p (a r t)")
+                out=hc[:].bitcast(FP8X4), scales=hs[:], in_=hgs[pr][:].rearrange("p a r t -> p (a r t)")
             )
-            h_codes[bt] = (hc, hs)
+            h_codes[pr] = (hc, hs)
 
         def mx(n):
-            bt = BATCH_OF[n // 2]
-            hc, hs = h_codes[bt]
-            first = n - 2 * BATCHES[bt][0]
-            tok = slice(P * first, P * (first + 1))
+            hc, hs = h_codes[n // 2]
+            tok = slice(P * (n % 2), P * (n % 2 + 1))
             pa = psum_a.tile([P, 512], F32)
             pb = psum_b.tile([P, 512], F32)
             for c, acc in enumerate((pa, pb)):
@@ -245,13 +254,20 @@ def tile_rawkvinjector_pa_t_kernel(
                     in1=u.unsqueeze(1).to_broadcast([P, 2, HD]),
                     op0=ALU.mult, op1=ALU.mult,
                 )
-            adder = nc.vector if n == n_tiles - 1 else nc.gpsimd
-            adder.tensor_tensor(
-                out=ob[:, 0:6, ii, :].rearrange("p k (s d) -> p k s d", s=2),
-                in0=z[:, :, 0, :].rearrange("p k (s d) -> p k s d", s=2),
-                in1=z[:, :, 1, :].rearrange("p k (s d) -> p k s d", s=2)[:, :, ::-1, :],
-                op=ALU.add,
-            )
+            def add(adder, h0, h1):
+                adder.tensor_tensor(
+                    out=ob[:, h0:h1, ii, :].rearrange("p k (s d) -> p k s d", s=2),
+                    in0=z[:, h0:h1, 0, :].rearrange("p k (s d) -> p k s d", s=2),
+                    in1=z[:, h0:h1, 1, :].rearrange("p k (s d) -> p k s d", s=2)[:, :, ::-1, :],
+                    op=ALU.add,
+                )
+
+            if n == n_tiles - 1:
+                add(nc.gpsimd, 0, 2)
+                add(nc.gpsimd, 2, 4)
+                add(nc.vector, 4, 6)
+            else:
+                add(nc.gpsimd, 0, 6)
             if n // GRP == n_tiles // GRP - 1:
                 store(n // GRP, ii, ii + 1)
             elif ii == GRP - 1:
@@ -261,44 +277,25 @@ def tile_rawkvinjector_pa_t_kernel(
             if 0 <= idx < limit:
                 f(idx)
 
-        stats(0)
         norm_weight_table()
-        norm(0)
-        transp(0)
-        stats(1)
-        norm(1)
-        stats(2)
-        weights()
-        evac(0)
-        transp(1)
-        quant(0)
-        mx(0)
-        mx(1)
-        build_table(0)
-        stats(3)
-        evac(1)
-        stats(4)
-        sq_heads(0)
-        build_table(1)
-        norm(2)
-        transp(2)
-        quant(1)
-        build_table(2)
-        evac(2)
-        norm(3)
-        transp(3)
-        build_table(3)
-        for j in range(n_pairs):
-            when(mx, 2 * j + 2, n_tiles)
-            when(sq_heads, 2 * j + 1, n_tiles)
-            when(rope, 2 * j, n_tiles)
-            when(mx, 2 * j + 3, n_tiles)
-            when(evac, j + 3, n_pairs)
-            when(norm, j + 4, n_pairs)
-            when(transp, j + 4, n_pairs)
-            when(sq_heads, 2 * j + 2, n_tiles)
-            when(rope, 2 * j + 1, n_tiles)
-            when(build_table, j + 4, TPP)
-            if j + 3 < n_pairs and j + 3 == BATCHES[BATCH_OF[j + 3]][-1]:
-                quant(BATCH_OF[j + 3])
-            when(stats, j + 5, n_pairs)
+        spread_q()
+        for n in range(-STATS_LEAD, n_tiles):
+            if n + NORM_LEAD == 2:
+                spread_kv()
+                quant_w(0)
+            if n + NORM_LEAD == 4:
+                quant_w(1)
+            when(mx, n + MX_LEAD, n_tiles)
+            if n % 2 == 0:
+                when(evac, (n + EVAC_LEAD) // 2, n_pairs)
+            when(sq_heads, n + MX_LEAD, n_tiles)
+            when(rope, n, n_tiles)
+            when(norm, n + NORM_LEAD, n_tiles)
+            if n % 2 == 1:
+                when(transp, (n + NORM_LEAD) // 2, n_pairs)
+                when(quant, (n - 1 + EVAC_LEAD) // 2, n_pairs)
+            when(stats, n + STATS_LEAD, n_tiles)
+            if n < 0:
+                when(build_table, n + TABLES_FIRST, TPP)
+            elif n % 2 == 1:
+                when(build_table, n // 2 + TABLES_FIRST, TPP)

@@ -290,10 +290,11 @@ def tile_rawkvinjector_pa_t_kernel(
                 when(evac, (n + EVAC_LEAD) // 2, n_pairs)
             when(sq_heads, n + MX_LEAD, n_tiles)
             when(rope, n, n_tiles)
+            if n % 2 == 1:
+                when(quant, (n - 1 + EVAC_LEAD) // 2, n_pairs)
             when(norm, n + NORM_LEAD, n_tiles)
             if n % 2 == 1:
                 when(transp, (n + NORM_LEAD) // 2, n_pairs)
-                when(quant, (n - 1 + EVAC_LEAD) // 2, n_pairs)
             when(stats, n + STATS_LEAD, n_tiles)
             if n < 0:
                 when(build_table, n + TABLES_FIRST, TPP)

@@ -30,7 +30,7 @@ def tile_rawkvinjector_pa_t_kernel(
     n_tiles = B * TPP
     n_pairs = n_tiles // 2
     MX_LEAD, EVAC_LEAD, NORM_LEAD, STATS_LEAD = 2, 4, 6, 10
-    TABLES_FIRST = 5
+    TABLES_FIRST = 4
     with ExitStack() as ctx:
         const = ctx.enter_context(tc.tile_pool(name="const", bufs=1))
         small = ctx.enter_context(tc.tile_pool(name="small", bufs=8))
@@ -56,12 +56,12 @@ def tile_rawkvinjector_pa_t_kernel(
         ones = const.tile([P, P], BF16)
         nc.vector.memset(ones[:], 1.0)
         warm = const.tile([P, 1], F32)
-        ident = const.tile([P, P], BF16)
+        ident = const.tile([P, P], F32)
         make_identity(nc, ident[:])
 
-        nc.scalar.dma_start(out=zrow[0:1, 0:D], in_=ln1_w.unsqueeze(0))
-        nc.scalar.dma_start(out=zrow[0:1, D : D + HD], in_=q_norm_w.unsqueeze(0))
-        nc.scalar.dma_start(out=zrow[0:1, D + HD : D + 2 * HD], in_=k_norm_w.unsqueeze(0))
+        nc.sync.dma_start(out=zrow[0:1, 0:D], in_=ln1_w.unsqueeze(0))
+        nc.sync.dma_start(out=zrow[0:1, D : D + HD], in_=q_norm_w.unsqueeze(0))
+        nc.sync.dma_start(out=zrow[0:1, D + HD : D + 2 * HD], in_=k_norm_w.unsqueeze(0))
         nc.scalar.activation(out=warm[:], in_=eps[:], func=ACT.Abs_reciprocal_sqrt)
         x_view = [hidden_states[b].rearrange("(p i) k -> p i k", i=TPP) for b in range(B)]
         x_sb = [const.tile([P, 2, D], BF16, name="x_%d" % pr) for pr in range(n_pairs)]
@@ -101,11 +101,8 @@ def tile_rawkvinjector_pa_t_kernel(
             out=wn_ps[:].rearrange("p a d -> p (a d)"), lhsT=ones[:], rhs=zrow[:, D : D + 2 * HD],
             start=True, stop=True,
         )
-        lnw_ps = psum_c.tile([P, 4, P], F32)
-        for t in range(4):
-            nc.tensor.matmul(
-                out=lnw_ps[:, t, :], lhsT=ones[:], rhs=zrow[:, t:D:4], start=True, stop=True
-            )
+        lnw_ps = psum_c.tile([P, D], F32)
+        nc.tensor.matmul(out=lnw_ps[:], lhsT=ones[:], rhs=zrow[:, 0:D], start=True, stop=True)
         wtab = const.tile([P, 2, 2, HD], BF16)
         tab = const.tile([P, TPP, 2, 2, HD], F32)
 
@@ -125,13 +122,6 @@ def tile_rawkvinjector_pa_t_kernel(
         wg = const.tile([P, NOUT, 4], BF16, align_bytes=64)
         wc = const.tile([P, NOUT], U32, align_bytes=64)
         ws = const.tile([P, NOUT], U8, align_bytes=64)
-
-        def spread_q():
-            interleave(wq_raw, 0, 512)
-
-        def spread_kv():
-            interleave(wk_raw, 512, 768)
-            interleave(wv_raw, 768, 1024)
 
         def interleave(raw, c0, c1):
             nc.vector.tensor_copy(
@@ -168,24 +158,25 @@ def tile_rawkvinjector_pa_t_kernel(
             if a == 0:
                 hs_[pr] = hpool.tile([P, 2, D], BF16, name="h")
             nc.vector.scalar_tensor_tensor(
-                out=hs_[pr][:, a, :].rearrange("p (t c) -> p t c", t=4),
-                in0=x_sb[pr][:, a, :].rearrange("p (c t) -> p t c", t=4),
+                out=hs_[pr][:, a, :], in0=x_sb[pr][:, a, :],
                 scalar=r0s[pr][1][:, a : a + 1], in1=lnw_ps[:],
                 op0=ALU.mult, op1=ALU.mult,
             )
 
         def transp(pr):
-            tp = psum_t.tile([P, 2, 4, P], BF16, tag="tp")
+            tp = psum_t.tile([P, 2, 2, P], F32, tag="tp")
             for a in range(2):
-                for t in range(4):
-                    nc.tensor.transpose(
-                        out=tp[:, a, t, :], in_=hs_[pr][:, a, P * t : P * (t + 1)], identity=ident[:]
-                    )
+                words = hs_[pr][:, a, :].bitcast(F32)
+                for u in range(2):
+                    nc.tensor.transpose(out=tp[:, a, u, :], in_=words[:, u : D // 2 : 2], identity=ident[:])
             tps[pr] = tp
 
         def evac(pr):
             hgs[pr] = hpool.tile([P, 2, P, 4], BF16, align_bytes=64, name="hg")
-            nc.scalar.copy(out=hgs[pr][:], in_=tps[pr][:].rearrange("p a t r -> p a r t"))
+            nc.scalar.copy(
+                out=hgs[pr][:].bitcast(F32),
+                in_=tps[pr][:].rearrange("p a u r -> p a r u"),
+            )
 
         def quant(pr):
             hc = codes.tile([P, 2 * P], U32, align_bytes=64)
@@ -278,12 +269,12 @@ def tile_rawkvinjector_pa_t_kernel(
                 f(idx)
 
         norm_weight_table()
-        spread_q()
+        interleave(wq_raw, 0, 512)
+        interleave(wk_raw, 512, 768)
+        interleave(wv_raw, 768, 1024)
         for n in range(-STATS_LEAD, n_tiles):
             if n + NORM_LEAD == 2:
-                spread_kv()
                 quant_w(0)
-            if n + NORM_LEAD == 4:
                 quant_w(1)
             when(mx, n + MX_LEAD, n_tiles)
             if n % 2 == 0:

@@ -29,7 +29,7 @@ def tile_rawkvinjector_pa_t_kernel(
     nc = tc.nc
     n_tiles = B * TPP
     n_pairs = n_tiles // 2
-    MX_LEAD, EVAC_LEAD, NORM_LEAD, STATS_LEAD = 2, 4, 6, 10
+    MX_LEAD, EVAC_LEAD, NORM_LEAD, STATS_LEAD = 2, 4, 6, 8
     TABLES_FIRST = 4
     with ExitStack() as ctx:
         const = ctx.enter_context(tc.tile_pool(name="const", bufs=1))
@@ -59,9 +59,6 @@ def tile_rawkvinjector_pa_t_kernel(
         ident = const.tile([P, P], F32)
         make_identity(nc, ident[:])
 
-        nc.sync.dma_start(out=zrow[0:1, 0:D], in_=ln1_w.unsqueeze(0))
-        nc.sync.dma_start(out=zrow[0:1, D : D + HD], in_=q_norm_w.unsqueeze(0))
-        nc.sync.dma_start(out=zrow[0:1, D + HD : D + 2 * HD], in_=k_norm_w.unsqueeze(0))
         nc.scalar.activation(out=warm[:], in_=eps[:], func=ACT.Abs_reciprocal_sqrt)
         x_view = [hidden_states[b].rearrange("(p i) k -> p i k", i=TPP) for b in range(B)]
         x_sb = [const.tile([P, 2, D], BF16, name="x_%d" % pr) for pr in range(n_pairs)]
@@ -84,11 +81,17 @@ def tile_rawkvinjector_pa_t_kernel(
             nc.sync.dma_start(out=cs_raw[:, 1, rows, 0:HALF], in_=sin_view[:, rows, HALF:HD])
             nc.sync.dma_start(out=cs_raw[:, 1, rows, HALF:HD], in_=sin_view[:, rows, 0:HALF])
 
-        nc.sync.dma_start(out=wq_raw[:], in_=Wq.rearrange("(p t) n -> p t n", t=4))
-        load_x(0)
+        wq_view = Wq.rearrange("(p t) n -> p t n", t=4)
+        nc.sync.dma_start(out=wq_raw[:, :, 0:256], in_=wq_view[:, :, 0:256])
+        nc.sync.dma_start(out=zrow[0:1, D : D + HD], in_=q_norm_w.unsqueeze(0))
+        nc.sync.dma_start(out=zrow[0:1, D + HD : D + 2 * HD], in_=k_norm_w.unsqueeze(0))
+        nc.sync.dma_start(out=zrow[0:1, 0:D], in_=ln1_w.unsqueeze(0))
+        for a in range(2):
+            nc.sync.dma_start(out=x_sb[0][:, a, :], in_=x_view[0][:, a, :])
+        nc.sync.dma_start(out=wq_raw[:, :, 256:512], in_=wq_view[:, :, 256:512])
+        load_x(1)
         nc.sync.dma_start(out=wk_raw[:], in_=Wk.rearrange("(p t) n -> p t n", t=4))
         nc.sync.dma_start(out=wv_raw[:], in_=Wv.rearrange("(p t) n -> p t n", t=4))
-        load_x(1)
         for g in range(TPP // GRP):
             load_cs(g)
             load_x(2 * g + 2)
@@ -107,14 +110,14 @@ def tile_rawkvinjector_pa_t_kernel(
         tab = const.tile([P, TPP, 2, 2, HD], F32)
 
         def norm_weight_table():
-            nc.scalar.copy(out=wtab[:, 0, :, :], in_=wn_ps[:])
-            nc.scalar.copy(out=wtab[:, 1, :, 0:HALF], in_=wn_ps[:, :, 0:HALF])
-            nc.scalar.mul(out=wtab[:, 1, :, HALF:HD], in_=wn_ps[:, :, HALF:HD], mul=-1.0)
+            nc.vector.tensor_copy(out=wtab[:, :, 0, :], in_=wn_ps[:])
+            nc.vector.tensor_copy(out=wtab[:, :, 1, 0:HALF], in_=wn_ps[:, :, 0:HALF])
+            nc.vector.tensor_scalar_mul(out=wtab[:, :, 1, HALF:HD], in0=wn_ps[:, :, HALF:HD], scalar1=-1.0)
 
         def build_table(i):
             nc.gpsimd.tensor_tensor(
-                out=tab[:, i, :, :, :].rearrange("p q c d -> p c q d"),
-                in0=cs_raw[:, :, i, :].unsqueeze(2).to_broadcast([P, 2, 2, HD]),
+                out=tab[:, i, :, :, :],
+                in0=cs_raw[:, :, i, :].unsqueeze(1).to_broadcast([P, 2, 2, HD]),
                 in1=wtab[:],
                 op=ALU.mult,
             )
@@ -126,7 +129,7 @@ def tile_rawkvinjector_pa_t_kernel(
         def interleave(raw, c0, c1):
             nc.vector.tensor_copy(
                 out=wg[:, c0:c1, :].rearrange("p (c i) t -> p c t i", i=4),
-                in_=raw[:].rearrange("p t (c i) -> p c t i", i=4),
+                in_=raw.rearrange("p t (c i) -> p c t i", i=4),
             )
 
         def quant_w(c):
@@ -268,26 +271,62 @@ def tile_rawkvinjector_pa_t_kernel(
             if 0 <= idx < limit:
                 f(idx)
 
+        interleave(wq_raw[:, :, 0:256], 0, 256)
         norm_weight_table()
-        interleave(wq_raw, 0, 512)
-        interleave(wk_raw, 512, 768)
-        interleave(wv_raw, 768, 1024)
-        for n in range(-STATS_LEAD, n_tiles):
-            if n + NORM_LEAD == 2:
-                quant_w(0)
-                quant_w(1)
+        interleave(wq_raw[:, :, 256:512], 256, 512)
+        for n in range(4):
+            stats(n)
+        norm(0)
+        norm(1)
+        transp(0)
+        interleave(wk_raw[:], 512, 768)
+        interleave(wv_raw[:], 768, 1024)
+        quant_w(0)
+        quant_w(1)
+        evac(0)
+        stats(4)
+        stats(5)
+        quant(0)
+        mx(0)
+        mx(1)
+        norm(2)
+        norm(3)
+        transp(1)
+        sq_heads(0)
+        evac(1)
+        norm(4)
+        norm(5)
+        transp(2)
+        sq_heads(1)
+        for i in range(TABLES_FIRST):
+            build_table(i)
+        rope(0)
+        quant(1)
+        mx(2)
+        evac(2)
+        stats(6)
+        stats(7)
+        sq_heads(2)
+        mx(3)
+        sq_heads(3)
+        rope(1)
+        quant(2)
+        norm(6)
+        norm(7)
+        transp(3)
+        build_table(TABLES_FIRST)
+        stats(8)
+        stats(9)
+        for n in range(2, n_tiles):
             when(mx, n + MX_LEAD, n_tiles)
             if n % 2 == 0:
                 when(evac, (n + EVAC_LEAD) // 2, n_pairs)
             when(sq_heads, n + MX_LEAD, n_tiles)
-            when(rope, n, n_tiles)
+            rope(n)
             if n % 2 == 1:
                 when(quant, (n - 1 + EVAC_LEAD) // 2, n_pairs)
             when(norm, n + NORM_LEAD, n_tiles)
             if n % 2 == 1:
                 when(transp, (n + NORM_LEAD) // 2, n_pairs)
-            when(stats, n + STATS_LEAD, n_tiles)
-            if n < 0:
-                when(build_table, n + TABLES_FIRST, TPP)
-            elif n % 2 == 1:
                 when(build_table, n // 2 + TABLES_FIRST, TPP)
+            when(stats, n + STATS_LEAD, n_tiles)

@@ -30,14 +30,14 @@ def tile_rawkvinjector_pa_t_kernel(
     n_tiles = B * TPP
     n_pairs = n_tiles // 2
     MX_LEAD, EVAC_LEAD, NORM_LEAD, STATS_LEAD = 2, 4, 6, 8
-    TABLES_FIRST = 4
+    TABLES_FIRST = 5
     with ExitStack() as ctx:
         const = ctx.enter_context(tc.tile_pool(name="const", bufs=1))
         small = ctx.enter_context(tc.tile_pool(name="small", bufs=8))
         junk = ctx.enter_context(tc.tile_pool(name="junk", bufs=4))
         hpool = ctx.enter_context(tc.tile_pool(name="hpool", bufs=3))
         codes = ctx.enter_context(tc.tile_pool(name="codes", bufs=4))
-        zpool = ctx.enter_context(tc.tile_pool(name="zpool", bufs=4))
+        zpool = ctx.enter_context(tc.tile_pool(name="zpool", bufs=3))
         obpool = ctx.enter_context(tc.tile_pool(name="obpool", bufs=3))
         psum_c = ctx.enter_context(tc.psum_pool(name="psum_c", bufs=1))
         psum_t = ctx.enter_context(tc.psum_pool(name="psum_t", bufs=1))
@@ -140,7 +140,7 @@ def tile_rawkvinjector_pa_t_kernel(
                 in_=wg[:, cols, :].rearrange("p n t -> p (n t)"),
             )
 
-        r0s, hs_, tps, hgs, h_codes, accs, rs, obs = {}, {}, {}, {}, {}, {}, {}, {}
+        r0s, hs_, tps, hgs, h_codes, accs, rs, obs, zs = {}, {}, {}, {}, {}, {}, {}, {}, {}
 
         def stats(n):
             pr, a = n // 2, n % 2
@@ -225,10 +225,12 @@ def tile_rawkvinjector_pa_t_kernel(
             )
             rs[n] = r
 
-        def store(grp, i0, i1):
+        Q_PART, K_PART, V_PART = (out_0, 0, NQ), (out_1, NQ, NQ + NK), (out_2, NQ + NK, NQ + NK + NV)
+
+        def store(grp, i0, i1, parts=(Q_PART, K_PART, V_PART)):
             b, g = grp % B, grp // B
             rows = slice(GRP * g + i0, GRP * g + i1)
-            for dst, h0, h1 in ((out_0, 0, 4), (out_1, 4, 6), (out_2, 6, 8)):
+            for dst, h0, h1 in parts:
                 nc.sync.dma_start(
                     out=dst[b].rearrange("h (p i) d -> p h i d", i=TPP)[:, :, rows, :],
                     in_=obs[grp][:, h0:h1, i0:i1, :],
@@ -240,32 +242,48 @@ def tile_rawkvinjector_pa_t_kernel(
             ob = obs[n // GRP]
             heads, pb = accs[n]
             r = rs[n]
-            z = zpool.tile([P, 6, 2, HD], F32)
-            for k, u in enumerate(heads):
+            if n % 2 == 0:
+                zs[n // 2] = zpool.tile([P, 2, NQ + NK, 2, HD], F32, name="z")
+            z = zs[n // 2]
+
+            def products(k):
                 qk = 0 if k < NQ else 1
                 nc.vector.scalar_tensor_tensor(
-                    out=z[:, k, :, :], in0=tab[:, i, qk, :, :], scalar=r[:, k : k + 1],
-                    in1=u.unsqueeze(1).to_broadcast([P, 2, HD]),
+                    out=z[:, :, k, n % 2, :], in0=tab[:, i, qk, :, :], scalar=r[:, k : k + 1],
+                    in1=heads[k].unsqueeze(1).to_broadcast([P, 2, HD]),
                     op0=ALU.mult, op1=ALU.mult,
                 )
-            def add(adder, h0, h1):
+
+            def add(adder, h0, h1, tiles=1):
+                a0, a1 = n % 2 + 1 - tiles, n % 2 + 1
                 adder.tensor_tensor(
-                    out=ob[:, h0:h1, ii, :].rearrange("p k (s d) -> p k s d", s=2),
-                    in0=z[:, h0:h1, 0, :].rearrange("p k (s d) -> p k s d", s=2),
-                    in1=z[:, h0:h1, 1, :].rearrange("p k (s d) -> p k s d", s=2)[:, :, ::-1, :],
+                    out=ob[:, h0:h1, ii + 1 - tiles : ii + 1, :].rearrange("p k a (s d) -> p k a s d", s=2),
+                    in0=z[:, 0, h0:h1, a0:a1, :].rearrange("p k a (s d) -> p k a s d", s=2),
+                    in1=z[:, 1, h0:h1, a0:a1, :].rearrange("p k a (s d) -> p k a s d", s=2)[:, :, :, ::-1, :],
                     op=ALU.add,
                 )
 
-            if n == n_tiles - 1:
-                add(nc.gpsimd, 0, 2)
-                add(nc.gpsimd, 2, 4)
-                add(nc.vector, 4, 6)
+            if n < n_tiles - 1:
+                for k in range(NQ + NK):
+                    products(k)
+                if n >= n_tiles - GRP:
+                    add(nc.gpsimd, 0, NQ + NK)
+                elif n % 2 == 1:
+                    add(nc.gpsimd, 0, NQ + NK, tiles=2)
+                if n // GRP == n_tiles // GRP - 1:
+                    store(n // GRP, ii, ii + 1)
+                elif ii == GRP - 1:
+                    store(n // GRP, 0, GRP)
             else:
-                add(nc.gpsimd, 0, 6)
-            if n // GRP == n_tiles // GRP - 1:
-                store(n // GRP, ii, ii + 1)
-            elif ii == GRP - 1:
-                store(n // GRP, 0, GRP)
+                store(n // GRP, ii, ii + 1, (V_PART,))
+                for k in range(NQ + 1):
+                    products(k)
+                add(nc.vector, 0, NQ)
+                store(n // GRP, ii, ii + 1, (Q_PART,))
+                for k in range(NQ + 1, NQ + NK):
+                    products(k)
+                add(nc.vector, NQ, NQ + NK)
+                store(n // GRP, ii, ii + 1, (K_PART,))
 
         def when(f, idx, limit):
             if 0 <= idx < limit:

@@ -29,8 +29,9 @@ def tile_rawkvinjector_pa_t_kernel(
     nc = tc.nc
     n_tiles = B * TPP
     n_pairs = n_tiles // 2
+    LAST = n_tiles // GRP - 1
     MX_LEAD, EVAC_LEAD, NORM_LEAD, STATS_LEAD = 2, 4, 6, 8
-    TABLES_FIRST = 5
+    TABLES_FIRST = 4
     with ExitStack() as ctx:
         const = ctx.enter_context(tc.tile_pool(name="const", bufs=1))
         small = ctx.enter_context(tc.tile_pool(name="small", bufs=8))
@@ -111,8 +112,11 @@ def tile_rawkvinjector_pa_t_kernel(
 
         def norm_weight_table():
             nc.vector.tensor_copy(out=wtab[:, :, 0, :], in_=wn_ps[:])
-            nc.vector.tensor_copy(out=wtab[:, :, 1, 0:HALF], in_=wn_ps[:, :, 0:HALF])
-            nc.vector.tensor_scalar_mul(out=wtab[:, :, 1, HALF:HD], in0=wn_ps[:, :, HALF:HD], scalar1=-1.0)
+            nc.vector.tensor_copy(out=wtab[:, :, 1, :], in_=wn_ps[:])
+
+        def negate_upper_sines():
+            upper = wtab[:, :, 1, HALF:HD]
+            nc.vector.tensor_scalar_mul(out=upper, in0=upper, scalar1=-1.0)
 
         def build_table(i):
             nc.gpsimd.tensor_tensor(
@@ -126,8 +130,8 @@ def tile_rawkvinjector_pa_t_kernel(
         wc = const.tile([P, NOUT], U32, align_bytes=64)
         ws = const.tile([P, NOUT], U8, align_bytes=64)
 
-        def interleave(raw, c0, c1):
-            nc.vector.tensor_copy(
+        def interleave(copy, raw, c0, c1):
+            copy(
                 out=wg[:, c0:c1, :].rearrange("p (c i) t -> p c t i", i=4),
                 in_=raw.rearrange("p t (c i) -> p c t i", i=4),
             )
@@ -206,6 +210,17 @@ def tile_rawkvinjector_pa_t_kernel(
             heads += [pb[:, HD * k : HD * (k + 1)] for k in range(NK)]
             accs[n] = (heads, pb)
 
+        Q_PART, K_PART, V_PART = (out_0, 0, NQ), (out_1, NQ, NQ + NK), (out_2, NQ + NK, NQ + NK + NV)
+
+        def store(grp, i0, i1, parts=(Q_PART, K_PART, V_PART), queue=nc.sync):
+            b, g = grp % B, grp // B
+            rows = slice(GRP * g + i0, GRP * g + i1)
+            for dst, h0, h1 in parts:
+                queue.dma_start(
+                    out=dst[b].rearrange("h (p i) d -> p h i d", i=TPP)[:, :, rows, :],
+                    in_=obs[grp][:, h0:h1, i0:i1, :],
+                )
+
         def sq_heads(n):
             b, g, ii = where(n)
             if ii == 0:
@@ -224,17 +239,8 @@ def tile_rawkvinjector_pa_t_kernel(
                 out=r[:], in_=ss[:], func=ACT.Abs_reciprocal_sqrt, scale=1.0 / HD, bias=eps[:, 0:1]
             )
             rs[n] = r
-
-        Q_PART, K_PART, V_PART = (out_0, 0, NQ), (out_1, NQ, NQ + NK), (out_2, NQ + NK, NQ + NK + NV)
-
-        def store(grp, i0, i1, parts=(Q_PART, K_PART, V_PART)):
-            b, g = grp % B, grp // B
-            rows = slice(GRP * g + i0, GRP * g + i1)
-            for dst, h0, h1 in parts:
-                nc.sync.dma_start(
-                    out=dst[b].rearrange("h (p i) d -> p h i d", i=TPP)[:, :, rows, :],
-                    in_=obs[grp][:, h0:h1, i0:i1, :],
-                )
+            if n // GRP == LAST and n % 2 == 1:
+                store(LAST, ii - 1, ii + 1, (V_PART,), nc.scalar)
 
         def rope(n):
             b, g, ii = where(n)
@@ -270,41 +276,43 @@ def tile_rawkvinjector_pa_t_kernel(
                     add(nc.gpsimd, 0, NQ + NK)
                 elif n % 2 == 1:
                     add(nc.gpsimd, 0, NQ + NK, tiles=2)
-                if n // GRP == n_tiles // GRP - 1:
-                    store(n // GRP, ii, ii + 1)
+                if n == n_tiles - 3:
+                    store(LAST, 0, 2, (Q_PART, K_PART))
+                elif n == n_tiles - 2:
+                    store(LAST, 2, 3, (Q_PART, K_PART))
                 elif ii == GRP - 1:
                     store(n // GRP, 0, GRP)
             else:
-                store(n // GRP, ii, ii + 1, (V_PART,))
                 for k in range(NQ + 1):
                     products(k)
                 add(nc.vector, 0, NQ)
-                store(n // GRP, ii, ii + 1, (Q_PART,))
+                store(LAST, ii, ii + 1, (Q_PART,))
                 for k in range(NQ + 1, NQ + NK):
                     products(k)
                 add(nc.vector, NQ, NQ + NK)
-                store(n // GRP, ii, ii + 1, (K_PART,))
+                store(LAST, ii, ii + 1, (K_PART,))
 
         def when(f, idx, limit):
             if 0 <= idx < limit:
                 f(idx)
 
-        interleave(wq_raw[:, :, 0:256], 0, 256)
+        interleave(nc.vector.tensor_copy, wq_raw[:, :, 0:256], 0, 256)
         norm_weight_table()
-        interleave(wq_raw[:, :, 256:512], 256, 512)
+        interleave(nc.vector.tensor_copy, wq_raw[:, :, 256:512], 256, 512)
         for n in range(4):
             stats(n)
         norm(0)
         norm(1)
         transp(0)
-        interleave(wk_raw[:], 512, 768)
-        interleave(wv_raw[:], 768, 1024)
+        interleave(nc.vector.tensor_copy, wk_raw[:], 512, 768)
+        interleave(nc.scalar.copy, wv_raw[:], 768, 1024)
         quant_w(0)
         quant_w(1)
         evac(0)
         stats(4)
         stats(5)
         quant(0)
+        negate_upper_sines()
         mx(0)
         mx(1)
         norm(2)
@@ -343,8 +351,9 @@ def tile_rawkvinjector_pa_t_kernel(
             rope(n)
             if n % 2 == 1:
                 when(quant, (n - 1 + EVAC_LEAD) // 2, n_pairs)
-            when(norm, n + NORM_LEAD, n_tiles)
             if n % 2 == 1:
+                when(norm, n + NORM_LEAD - 1, n_tiles)
+                when(norm, n + NORM_LEAD, n_tiles)
                 when(transp, (n + NORM_LEAD) // 2, n_pairs)
                 when(build_table, n // 2 + TABLES_FIRST, TPP)
             when(stats, n + STATS_LEAD, n_tiles)

@@ -29,14 +29,12 @@ def tile_rawkvinjector_pa_t_kernel(
     nc = tc.nc
     n_tiles = B * TPP
     n_pairs = n_tiles // 2
-    LAST = n_tiles // GRP - 1
-    MX_LEAD, EVAC_LEAD, NORM_LEAD, STATS_LEAD = 2, 4, 6, 8
-    TABLES_FIRST = 4
     with ExitStack() as ctx:
         const = ctx.enter_context(tc.tile_pool(name="const", bufs=1))
         small = ctx.enter_context(tc.tile_pool(name="small", bufs=8))
         junk = ctx.enter_context(tc.tile_pool(name="junk", bufs=4))
-        hpool = ctx.enter_context(tc.tile_pool(name="hpool", bufs=3))
+        hpool = ctx.enter_context(tc.tile_pool(name="hpool", bufs=5))
+        hgpool = ctx.enter_context(tc.tile_pool(name="hgpool", bufs=3))
         codes = ctx.enter_context(tc.tile_pool(name="codes", bufs=4))
         zpool = ctx.enter_context(tc.tile_pool(name="zpool", bufs=3))
         obpool = ctx.enter_context(tc.tile_pool(name="obpool", bufs=3))
@@ -72,33 +70,45 @@ def tile_rawkvinjector_pa_t_kernel(
         wq_raw = const.tile([P, 4, NQ * HD], BF16)
         wk_raw = const.tile([P, 4, NK * HD], BF16)
         wv_raw = const.tile([P, 4, NV * HD], BF16)
-        cs_raw = const.tile([P, 2, TPP, HD], BF16)
+        cs_raw = const.tile([P, TPP, 2, HD], BF16)
         cos_view = cos.rearrange("(p i) d -> p i d", i=TPP)
         sin_view = sin.rearrange("(p i) d -> p i d", i=TPP)
 
         def load_cs(g):
             rows = slice(GRP * g, GRP * (g + 1))
-            nc.sync.dma_start(out=cs_raw[:, 0, rows, :], in_=cos_view[:, rows, :])
-            nc.sync.dma_start(out=cs_raw[:, 1, rows, 0:HALF], in_=sin_view[:, rows, HALF:HD])
-            nc.sync.dma_start(out=cs_raw[:, 1, rows, HALF:HD], in_=sin_view[:, rows, 0:HALF])
+            nc.sync.dma_start(out=cs_raw[:, rows, 0, :], in_=cos_view[:, rows, :])
+            nc.sync.dma_start(out=cs_raw[:, rows, 1, 0:HALF], in_=sin_view[:, rows, HALF:HD])
+            nc.sync.dma_start(out=cs_raw[:, rows, 1, HALF:HD], in_=sin_view[:, rows, 0:HALF])
 
         wq_view = Wq.rearrange("(p t) n -> p t n", t=4)
+        nc.sync.dma_start(out=x_sb[0][:, 0, :], in_=x_view[0][:, 0, :])
         nc.sync.dma_start(out=wq_raw[:, :, 0:256], in_=wq_view[:, :, 0:256])
+        nc.sync.dma_start(out=x_sb[0][:, 1, :], in_=x_view[0][:, 1, :])
         nc.sync.dma_start(out=zrow[0:1, D : D + HD], in_=q_norm_w.unsqueeze(0))
         nc.sync.dma_start(out=zrow[0:1, D + HD : D + 2 * HD], in_=k_norm_w.unsqueeze(0))
         nc.sync.dma_start(out=zrow[0:1, 0:D], in_=ln1_w.unsqueeze(0))
-        for a in range(2):
-            nc.sync.dma_start(out=x_sb[0][:, a, :], in_=x_view[0][:, a, :])
         nc.sync.dma_start(out=wq_raw[:, :, 256:512], in_=wq_view[:, :, 256:512])
         load_x(1)
         nc.sync.dma_start(out=wk_raw[:], in_=Wk.rearrange("(p t) n -> p t n", t=4))
         nc.sync.dma_start(out=wv_raw[:], in_=Wv.rearrange("(p t) n -> p t n", t=4))
-        for g in range(TPP // GRP):
-            load_cs(g)
-            load_x(2 * g + 2)
-            load_x(2 * g + 3)
-        for pr in range(2 * (TPP // GRP) + 2, n_pairs):
-            load_x(pr)
+        load_cs(0)
+        load_x(2)
+        load_x(3)
+        load_cs(1)
+        load_x(4)
+        load_x(5)
+        load_cs(2)
+        load_x(6)
+        load_x(7)
+        load_cs(3)
+        load_x(8)
+        load_x(9)
+        load_x(10)
+        load_x(11)
+        load_x(12)
+        load_x(13)
+        load_x(14)
+        load_x(15)
 
         wn_ps = psum_t.tile([P, 2, HD], F32, tag="tp")
         nc.tensor.matmul(
@@ -118,11 +128,15 @@ def tile_rawkvinjector_pa_t_kernel(
             upper = wtab[:, :, 1, HALF:HD]
             nc.vector.tensor_scalar_mul(out=upper, in0=upper, scalar1=-1.0)
 
-        def build_table(i):
-            nc.gpsimd.tensor_tensor(
-                out=tab[:, i, :, :, :],
-                in0=cs_raw[:, :, i, :].unsqueeze(1).to_broadcast([P, 2, 2, HD]),
-                in1=wtab[:],
+        def build_tables(i0, count, engine=nc.gpsimd):
+            shape = [P, count, 2, 2 * HD]
+            engine.tensor_tensor(
+                out=tab[:, i0 : i0 + count, :, :, :].rearrange("p i w s d -> p i w (s d)"),
+                in0=cs_raw[:, i0 : i0 + count, :, :]
+                .rearrange("p i s d -> p i (s d)")
+                .unsqueeze(2)
+                .to_broadcast(shape),
+                in1=wtab[:].rearrange("p w s d -> p w (s d)").unsqueeze(1).to_broadcast(shape),
                 op=ALU.mult,
             )
 
@@ -144,21 +158,22 @@ def tile_rawkvinjector_pa_t_kernel(
                 in_=wg[:, cols, :].rearrange("p n t -> p (n t)"),
             )
 
-        r0s, hs_, tps, hgs, h_codes, accs, rs, obs, zs = {}, {}, {}, {}, {}, {}, {}, {}, {}
+        r0s, hs_, tps, hgs, h_codes, banks, rs, obs, zs = {}, {}, {}, {}, {}, {}, {}, {}, {}
 
         def stats(n):
             pr, a = n // 2, n % 2
             if a == 0:
                 r0s[pr] = small.tile([P, 2], F32, name="ss0"), small.tile([P, 2], F32, name="r0")
-            ss0, r0 = r0s[pr]
             sq = junk.tile([P, D], BF16)
             nc.scalar.activation(
-                out=sq[:], in_=x_sb[pr][:, a, :], func=ACT.Square, accum_out=ss0[:, a : a + 1]
+                out=sq[:], in_=x_sb[pr][:, a, :], func=ACT.Square, accum_out=r0s[pr][0][:, a : a + 1]
             )
-            if a == 1:
-                nc.scalar.activation(
-                    out=r0[:], in_=ss0[:], func=ACT.Abs_reciprocal_sqrt, scale=1.0 / D, bias=eps[:, 0:1]
-                )
+
+        def token_scale(pr):
+            ss0, r0 = r0s[pr]
+            nc.scalar.activation(
+                out=r0[:], in_=ss0[:], func=ACT.Abs_reciprocal_sqrt, scale=1.0 / D, bias=eps[:, 0:1]
+            )
 
         def norm(n):
             pr, a = n // 2, n % 2
@@ -178,37 +193,51 @@ def tile_rawkvinjector_pa_t_kernel(
                     nc.tensor.transpose(out=tp[:, a, u, :], in_=words[:, u : D // 2 : 2], identity=ident[:])
             tps[pr] = tp
 
+        def codes_place(pr):
+            if pr < PAIR_CALLS:
+                return pr, 1
+            return pr - (pr - PAIR_CALLS) % 2, 2
+
         def evac(pr):
-            hgs[pr] = hpool.tile([P, 2, P, 4], BF16, align_bytes=64, name="hg")
+            first, count = codes_place(pr)
+            if pr == first:
+                hgs[first] = hgpool.tile([P, 2 * count, P, 4], BF16, align_bytes=64, name="hg%d" % count)
+            a0 = 2 * (pr - first)
             nc.scalar.copy(
-                out=hgs[pr][:].bitcast(F32),
+                out=hgs[first][:, a0 : a0 + 2, :, :].bitcast(F32),
                 in_=tps[pr][:].rearrange("p a u r -> p a r u"),
             )
 
-        def quant(pr):
-            hc = codes.tile([P, 2 * P], U32, align_bytes=64)
-            hs = codes.tile([P, 2 * P], U8, align_bytes=64)
+        def quant(first):
+            count = codes_place(first)[1]
+            hc = codes.tile([P, 2 * P * count], U32, align_bytes=64, name="hc%d" % count)
+            hs = codes.tile([P, 2 * P * count], U8, align_bytes=64, name="hs%d" % count)
             nc.vector.quantize_mx(
-                out=hc[:].bitcast(FP8X4), scales=hs[:], in_=hgs[pr][:].rearrange("p a r t -> p (a r t)")
+                out=hc[:].bitcast(FP8X4), scales=hs[:], in_=hgs[first][:].rearrange("p a r t -> p (a r t)")
             )
-            h_codes[pr] = (hc, hs)
+            h_codes[first] = (hc, hs)
 
-        def mx(n):
-            hc, hs = h_codes[n // 2]
-            tok = slice(P * (n % 2), P * (n % 2 + 1))
-            pa = psum_a.tile([P, 512], F32)
-            pb = psum_b.tile([P, 512], F32)
-            for c, acc in enumerate((pa, pb)):
+        def mx(n, parts=(0, 1)):
+            first = codes_place(n // 2)[0]
+            hc, hs = h_codes[first]
+            a = n - 2 * first
+            tok = slice(P * a, P * (a + 1))
+            if 0 in parts:
+                pa = psum_a.tile([P, 512], F32, name="pa")
+                pb = psum_b.tile([P, 512], F32, name="pb")
+                banks[n] = (pa, pb)
+            for c in parts:
                 cols = slice(512 * c, 512 * (c + 1))
                 nc.tensor.matmul_mx(
-                    out=acc[:],
+                    out=banks[n][c][:],
                     lhsT=hc[:, tok].bitcast(FP8X4), lhsT_scale=hs[:, tok],
                     rhs=wc[:, cols].bitcast(FP8X4), rhs_scale=ws[:, cols],
                     start=True, stop=True,
                 )
-            heads = [pa[:, HD * k : HD * (k + 1)] for k in range(NQ)]
-            heads += [pb[:, HD * k : HD * (k + 1)] for k in range(NK)]
-            accs[n] = (heads, pb)
+
+        def head(n, k):
+            pa, pb = banks[n]
+            return pa[:, HD * k : HD * (k + 1)] if k < NQ else pb[:, HD * (k - NQ) : HD * (k - NQ + 1)]
 
         Q_PART, K_PART, V_PART = (out_0, 0, NQ), (out_1, NQ, NQ + NK), (out_2, NQ + NK, NQ + NK + NV)
 
@@ -226,134 +255,134 @@ def tile_rawkvinjector_pa_t_kernel(
             if ii == 0:
                 obs[n // GRP] = obpool.tile([P, 8, GRP, HD], F32, name="ob")
             ob = obs[n // GRP]
-            heads, pb = accs[n]
             ss = small.tile([P, 6], F32)
-            for k, u in enumerate(heads):
+            for k in range(NQ + NK):
                 sq1 = junk.tile([P, HD], BF16)
-                nc.scalar.activation(out=sq1[:], in_=u, func=ACT.Square, accum_out=ss[:, k : k + 1])
+                nc.scalar.activation(out=sq1[:], in_=head(n, k), func=ACT.Square, accum_out=ss[:, k : k + 1])
             nc.scalar.copy(
-                out=ob[:, 6:8, ii, :], in_=pb[:, 256:512].rearrange("p (h d) -> p h d", h=2)
+                out=ob[:, 6:8, ii, :], in_=banks[n][1][:, 256:512].rearrange("p (h d) -> p h d", h=2)
             )
             r = small.tile([P, 6], F32)
             nc.scalar.activation(
                 out=r[:], in_=ss[:], func=ACT.Abs_reciprocal_sqrt, scale=1.0 / HD, bias=eps[:, 0:1]
             )
             rs[n] = r
-            if n // GRP == LAST and n % 2 == 1:
-                store(LAST, ii - 1, ii + 1, (V_PART,), nc.scalar)
 
-        def rope(n):
+        def rope(n, k0=0, k1=NQ + NK):
             b, g, ii = where(n)
-            i = GRP * g + ii
-            ob = obs[n // GRP]
-            heads, pb = accs[n]
-            r = rs[n]
-            if n % 2 == 0:
+            if n % 2 == 0 and k0 == 0:
                 zs[n // 2] = zpool.tile([P, 2, NQ + NK, 2, HD], F32, name="z")
             z = zs[n // 2]
-
-            def products(k):
-                qk = 0 if k < NQ else 1
+            for k in range(k0, k1):
                 nc.vector.scalar_tensor_tensor(
-                    out=z[:, :, k, n % 2, :], in0=tab[:, i, qk, :, :], scalar=r[:, k : k + 1],
-                    in1=heads[k].unsqueeze(1).to_broadcast([P, 2, HD]),
+                    out=z[:, :, k, n % 2, :], in0=tab[:, GRP * g + ii, 0 if k < NQ else 1, :, :],
+                    scalar=rs[n][:, k : k + 1],
+                    in1=head(n, k).unsqueeze(1).to_broadcast([P, 2, HD]),
                     op0=ALU.mult, op1=ALU.mult,
                 )
 
-            def add(adder, h0, h1, tiles=1):
-                a0, a1 = n % 2 + 1 - tiles, n % 2 + 1
-                adder.tensor_tensor(
-                    out=ob[:, h0:h1, ii + 1 - tiles : ii + 1, :].rearrange("p k a (s d) -> p k a s d", s=2),
-                    in0=z[:, 0, h0:h1, a0:a1, :].rearrange("p k a (s d) -> p k a s d", s=2),
-                    in1=z[:, 1, h0:h1, a0:a1, :].rearrange("p k a (s d) -> p k a s d", s=2)[:, :, :, ::-1, :],
-                    op=ALU.add,
-                )
+        def add(n, tiles=1, engine=nc.gpsimd, h0=0, h1=NQ + NK):
+            ii = n % GRP
+            z, ob = zs[n // 2], obs[n // GRP]
+            a0, a1 = n % 2, n % 2 + tiles
+            engine.tensor_tensor(
+                out=ob[:, h0:h1, ii : ii + tiles, :].rearrange("p k a (s d) -> p k a s d", s=2),
+                in0=z[:, 0, h0:h1, a0:a1, :].rearrange("p k a (s d) -> p k a s d", s=2),
+                in1=z[:, 1, h0:h1, a0:a1, :].rearrange("p k a (s d) -> p k a s d", s=2)[:, :, :, ::-1, :],
+                op=ALU.add,
+            )
 
-            if n < n_tiles - 1:
-                for k in range(NQ + NK):
-                    products(k)
-                if n >= n_tiles - GRP:
-                    add(nc.gpsimd, 0, NQ + NK)
-                elif n % 2 == 1:
-                    add(nc.gpsimd, 0, NQ + NK, tiles=2)
-                if n == n_tiles - 3:
-                    store(LAST, 0, 2, (Q_PART, K_PART))
-                elif n == n_tiles - 2:
-                    store(LAST, 2, 3, (Q_PART, K_PART))
-                elif ii == GRP - 1:
-                    store(n // GRP, 0, GRP)
-            else:
-                for k in range(NQ + 1):
-                    products(k)
-                add(nc.vector, 0, NQ)
-                store(LAST, ii, ii + 1, (Q_PART,))
-                for k in range(NQ + 1, NQ + NK):
-                    products(k)
-                add(nc.vector, NQ, NQ + NK)
-                store(LAST, ii, ii + 1, (K_PART,))
-
-        def when(f, idx, limit):
+        def when(f, idx, limit, *rest):
             if 0 <= idx < limit:
-                f(idx)
+                f(idx, *rest)
 
+        PAIR_CALLS = n_pairs
+        PAIR_STORES = 20
+        stats(0)
+        stats(1)
+        token_scale(0)
+        stats(2)
+        stats(3)
+        token_scale(1)
         interleave(nc.vector.tensor_copy, wq_raw[:, :, 0:256], 0, 256)
-        norm_weight_table()
         interleave(nc.vector.tensor_copy, wq_raw[:, :, 256:512], 256, 512)
-        for n in range(4):
-            stats(n)
         norm(0)
         norm(1)
+        norm_weight_table()
         transp(0)
-        interleave(nc.vector.tensor_copy, wk_raw[:], 512, 768)
         interleave(nc.scalar.copy, wv_raw[:], 768, 1024)
-        quant_w(0)
-        quant_w(1)
         evac(0)
         stats(4)
         stats(5)
-        quant(0)
-        negate_upper_sines()
-        mx(0)
-        mx(1)
+        token_scale(2)
+        quant_w(0)
+        interleave(nc.vector.tensor_copy, wk_raw[:], 512, 768)
         norm(2)
+        quant(0)
+        mx(0, (0,))
+        quant_w(1)
+        mx(0, (1,))
+        mx(1)
+        negate_upper_sines()
+        for i in range(4):
+            build_tables(i, 1)
         norm(3)
         transp(1)
         sq_heads(0)
-        evac(1)
         norm(4)
         norm(5)
         transp(2)
+        stats(6)
+        evac(1)
         sq_heads(1)
-        for i in range(TABLES_FIRST):
-            build_table(i)
         rope(0)
         quant(1)
         mx(2)
-        evac(2)
-        stats(6)
-        stats(7)
-        sq_heads(2)
         mx(3)
-        sq_heads(3)
+        stats(7)
+        evac(2)
+        token_scale(3)
         rope(1)
         quant(2)
+        add(0, 2)
         norm(6)
         norm(7)
         transp(3)
-        build_table(TABLES_FIRST)
+        sq_heads(2)
+        sq_heads(3)
+        build_tables(4, 1)
         stats(8)
         stats(9)
+
         for n in range(2, n_tiles):
-            when(mx, n + MX_LEAD, n_tiles)
+            grp, place = n // GRP, n % GRP
+            when(mx, n + 2, n_tiles)
             if n % 2 == 0:
-                when(evac, (n + EVAC_LEAD) // 2, n_pairs)
-            when(sq_heads, n + MX_LEAD, n_tiles)
+                when(evac, n // 2 + 2, n_pairs)
+                when(token_scale, n // 2 + 3, n_pairs)
+            when(sq_heads, n + 2, n_tiles)
+            if n % 2 == 1 and PAIR_STORES <= n + 1 < n_tiles - 1:
+                store((n + 2) // GRP, (n + 1) % GRP, (n + 1) % GRP + 2, (V_PART,), nc.scalar)
             rope(n)
             if n % 2 == 1:
-                when(quant, (n - 1 + EVAC_LEAD) // 2, n_pairs)
-            if n % 2 == 1:
-                when(norm, n + NORM_LEAD - 1, n_tiles)
-                when(norm, n + NORM_LEAD, n_tiles)
-                when(transp, (n + NORM_LEAD) // 2, n_pairs)
-                when(build_table, n // 2 + TABLES_FIRST, TPP)
-            when(stats, n + STATS_LEAD, n_tiles)
+                when(quant, (n + 3) // 2, n_pairs)
+                if n < 28:
+                    add(n - 1, 2)
+                when(norm, n + 5, n_tiles)
+                when(norm, n + 6, n_tiles)
+                when(transp, (n + 5) // 2, n_pairs)
+                when(build_tables, n // 2 + 4, TPP, 1)
+                if PAIR_STORES <= n < 28:
+                    store(grp, place - 1, place + 1, (Q_PART, K_PART))
+            if n in (28, 29):
+                add(n)
+                store(grp, place, place + 1, (Q_PART, K_PART))
+            if place == 3 and n < PAIR_STORES:
+                store(grp, 0, GRP)
+            when(stats, n + 8, n_tiles)
+        add(30, 1, nc.vector)
+        store(7, 2, 3, (Q_PART, K_PART))
+        add(31, 1, nc.vector, 0, NQ)
+        store(7, 3, 4, (Q_PART,))
+        add(31, 1, nc.vector, NQ, NQ + NK)
+        store(7, 3, 4, (K_PART,))

@@ -37,7 +37,7 @@ def tile_rawkvinjector_pa_t_kernel(
         hgpool = ctx.enter_context(tc.tile_pool(name="hgpool", bufs=3))
         codes = ctx.enter_context(tc.tile_pool(name="codes", bufs=4))
         zpool = ctx.enter_context(tc.tile_pool(name="zpool", bufs=3))
-        obpool = ctx.enter_context(tc.tile_pool(name="obpool", bufs=3))
+        obpool = ctx.enter_context(tc.tile_pool(name="obpool", bufs=8))
         psum_c = ctx.enter_context(tc.psum_pool(name="psum_c", bufs=1))
         psum_t = ctx.enter_context(tc.psum_pool(name="psum_t", bufs=1))
         psum_a = ctx.enter_context(tc.psum_pool(name="psum_a", bufs=3))
@@ -241,26 +241,25 @@ def tile_rawkvinjector_pa_t_kernel(
 
         Q_PART, K_PART, V_PART = (out_0, 0, NQ), (out_1, NQ, NQ + NK), (out_2, NQ + NK, NQ + NK + NV)
 
-        def store(grp, i0, i1, parts=(Q_PART, K_PART, V_PART), queue=nc.sync):
-            b, g = grp % B, grp // B
-            rows = slice(GRP * g + i0, GRP * g + i1)
+        def store(n, tiles=2, parts=(Q_PART, K_PART, V_PART), queue=nc.sync):
+            b, g, ii = where(n)
+            rows = slice(GRP * g + ii, GRP * g + ii + tiles)
             for dst, h0, h1 in parts:
                 queue.dma_start(
                     out=dst[b].rearrange("h (p i) d -> p h i d", i=TPP)[:, :, rows, :],
-                    in_=obs[grp][:, h0:h1, i0:i1, :],
+                    in_=obs[n // 2][:, h0:h1, n % 2 : n % 2 + tiles, :],
                 )
 
         def sq_heads(n):
-            b, g, ii = where(n)
-            if ii == 0:
-                obs[n // GRP] = obpool.tile([P, 8, GRP, HD], F32, name="ob")
-            ob = obs[n // GRP]
+            if n % 2 == 0:
+                obs[n // 2] = obpool.tile([P, 8, 2, HD], F32, name="ob")
+            ob = obs[n // 2]
             ss = small.tile([P, 6], F32)
             for k in range(NQ + NK):
                 sq1 = junk.tile([P, HD], BF16)
                 nc.scalar.activation(out=sq1[:], in_=head(n, k), func=ACT.Square, accum_out=ss[:, k : k + 1])
             nc.scalar.copy(
-                out=ob[:, 6:8, ii, :], in_=banks[n][1][:, 256:512].rearrange("p (h d) -> p h d", h=2)
+                out=ob[:, 6:8, n % 2, :], in_=banks[n][1][:, 256:512].rearrange("p (h d) -> p h d", h=2)
             )
             r = small.tile([P, 6], F32)
             nc.scalar.activation(
@@ -282,11 +281,10 @@ def tile_rawkvinjector_pa_t_kernel(
                 )
 
         def add(n, tiles=1, engine=nc.gpsimd, h0=0, h1=NQ + NK):
-            ii = n % GRP
-            z, ob = zs[n // 2], obs[n // GRP]
+            z, ob = zs[n // 2], obs[n // 2]
             a0, a1 = n % 2, n % 2 + tiles
             engine.tensor_tensor(
-                out=ob[:, h0:h1, ii : ii + tiles, :].rearrange("p k a (s d) -> p k a s d", s=2),
+                out=ob[:, h0:h1, a0:a1, :].rearrange("p k a (s d) -> p k a s d", s=2),
                 in0=z[:, 0, h0:h1, a0:a1, :].rearrange("p k a (s d) -> p k a s d", s=2),
                 in1=z[:, 1, h0:h1, a0:a1, :].rearrange("p k a (s d) -> p k a s d", s=2)[:, :, :, ::-1, :],
                 op=ALU.add,
@@ -297,7 +295,6 @@ def tile_rawkvinjector_pa_t_kernel(
                 f(idx, *rest)
 
         PAIR_CALLS = n_pairs
-        PAIR_STORES = 20
         stats(0)
         stats(1)
         token_scale(0)
@@ -345,24 +342,25 @@ def tile_rawkvinjector_pa_t_kernel(
         rope(1)
         quant(2)
         add(0, 2)
+        store(0)
         norm(6)
         norm(7)
         transp(3)
         sq_heads(2)
         sq_heads(3)
+        store(2, 2, (V_PART,))
         build_tables(4, 1)
         stats(8)
         stats(9)
 
         for n in range(2, n_tiles):
-            grp, place = n // GRP, n % GRP
             when(mx, n + 2, n_tiles)
             if n % 2 == 0:
                 when(evac, n // 2 + 2, n_pairs)
                 when(token_scale, n // 2 + 3, n_pairs)
             when(sq_heads, n + 2, n_tiles)
-            if n % 2 == 1 and PAIR_STORES <= n + 1 < n_tiles - 1:
-                store((n + 2) // GRP, (n + 1) % GRP, (n + 1) % GRP + 2, (V_PART,), nc.scalar)
+            if n % 2 == 1 and n + 2 < n_tiles:
+                store(n + 1, 2, (V_PART,), nc.sync if n < 19 else nc.scalar)
             rope(n)
             if n % 2 == 1:
                 when(quant, (n + 3) // 2, n_pairs)
@@ -372,17 +370,15 @@ def tile_rawkvinjector_pa_t_kernel(
                 when(norm, n + 6, n_tiles)
                 when(transp, (n + 5) // 2, n_pairs)
                 when(build_tables, n // 2 + 4, TPP, 1)
-                if PAIR_STORES <= n < 28:
-                    store(grp, place - 1, place + 1, (Q_PART, K_PART))
+                if n < 28:
+                    store(n - 1, 2, (Q_PART, K_PART))
             if n in (28, 29):
                 add(n)
-                store(grp, place, place + 1, (Q_PART, K_PART))
-            if place == 3 and n < PAIR_STORES:
-                store(grp, 0, GRP)
+                store(n, 1, (Q_PART, K_PART))
             when(stats, n + 8, n_tiles)
         add(30, 1, nc.vector)
-        store(7, 2, 3, (Q_PART, K_PART))
+        store(30, 1, (Q_PART, K_PART))
         add(31, 1, nc.vector, 0, NQ)
-        store(7, 3, 4, (Q_PART,))
+        store(31, 1, (Q_PART,))
         add(31, 1, nc.vector, NQ, NQ + NK)
-        store(7, 3, 4, (K_PART,))
+        store(31, 1, (K_PART,))

from contextlib import ExitStack

import concourse.mybir as mybir
from concourse.masks import make_identity

F32 = mybir.dt.float32
BF16 = mybir.dt.bfloat16
U32 = mybir.dt.uint32
U8 = mybir.dt.uint8
FP8X4 = mybir.dt.float8_e4m3fn_x4
ALU = mybir.AluOpType
ACT = mybir.ActivationFunctionType

P = 128
B, T, D = 2, 2048, 512
HD = 128
HALF = 64
NQ, NK, NV = 4, 2, 2
NOUT = (NQ + NK + NV) * HD
TPP = T // P
GRP = 4
EPS = 1e-6
FLOPS = 2 * B * T * D * NOUT


def tile_rawkvinjector_pa_t_kernel(
    tc, hidden_states, ln1_w, Wq, Wk, Wv, q_norm_w, k_norm_w, cos, sin, out_0, out_1, out_2
):
    nc = tc.nc
    n_tiles = B * TPP
    n_pairs = n_tiles // 2
    with ExitStack() as ctx:
        const = ctx.enter_context(tc.tile_pool(name="const", bufs=1))
        small = ctx.enter_context(tc.tile_pool(name="small", bufs=8))
        junk = ctx.enter_context(tc.tile_pool(name="junk", bufs=4))
        hpool = ctx.enter_context(tc.tile_pool(name="hpool", bufs=5))
        hgpool = ctx.enter_context(tc.tile_pool(name="hgpool", bufs=3))
        codes = ctx.enter_context(tc.tile_pool(name="codes", bufs=4))
        zpool = ctx.enter_context(tc.tile_pool(name="zpool", bufs=3))
        obpool = ctx.enter_context(tc.tile_pool(name="obpool", bufs=8))
        psum_c = ctx.enter_context(tc.psum_pool(name="psum_c", bufs=1))
        psum_t = ctx.enter_context(tc.psum_pool(name="psum_t", bufs=1))
        psum_a = ctx.enter_context(tc.psum_pool(name="psum_a", bufs=3))
        psum_b = ctx.enter_context(tc.psum_pool(name="psum_b", bufs=3))
        ctx.enter_context(tc.manual_schedule())

        def where(n):
            grp = n // GRP
            return grp % B, grp // B, n % GRP

        zrow = const.tile([P, D + 2 * HD], BF16)
        nc.gpsimd.memset(zrow[:].bitcast(U32), 0)
        eps = const.tile([P, 1], F32)
        nc.vector.memset(eps[:], EPS)
        ones = const.tile([P, P], BF16)
        nc.vector.memset(ones[:], 1.0)
        warm = const.tile([P, 1], F32)
        ident = const.tile([P, P], F32)
        make_identity(nc, ident[:])

        nc.scalar.activation(out=warm[:], in_=eps[:], func=ACT.Abs_reciprocal_sqrt)
        x_view = [hidden_states[b].rearrange("(p i) k -> p i k", i=TPP) for b in range(B)]
        x_sb = [const.tile([P, 2, D], BF16, name="x_%d" % pr) for pr in range(n_pairs)]

        def load_x(pr):
            b, g, ii = where(2 * pr)
            i = GRP * g + ii
            nc.sync.dma_start(out=x_sb[pr][:], in_=x_view[b][:, i : i + 2, :])

        wq_raw = const.tile([P, 4, NQ * HD], BF16)
        wk_raw = const.tile([P, 4, NK * HD], BF16)
        wv_raw = const.tile([P, 4, NV * HD], BF16)
        cs_raw = const.tile([P, TPP, 2, HD], BF16)
        cos_view = cos.rearrange("(p i) d -> p i d", i=TPP)
        sin_view = sin.rearrange("(p i) d -> p i d", i=TPP)

        def load_cs(g):
            rows = slice(GRP * g, GRP * (g + 1))
            nc.sync.dma_start(out=cs_raw[:, rows, 0, :], in_=cos_view[:, rows, :])
            nc.sync.dma_start(out=cs_raw[:, rows, 1, 0:HALF], in_=sin_view[:, rows, HALF:HD])
            nc.sync.dma_start(out=cs_raw[:, rows, 1, HALF:HD], in_=sin_view[:, rows, 0:HALF])

        wq_view = Wq.rearrange("(p t) n -> p t n", t=4)
        nc.sync.dma_start(out=x_sb[0][:, 0, :], in_=x_view[0][:, 0, :])
        nc.sync.dma_start(out=wq_raw[:, :, 0:256], in_=wq_view[:, :, 0:256])
        nc.sync.dma_start(out=x_sb[0][:, 1, :], in_=x_view[0][:, 1, :])
        nc.sync.dma_start(out=zrow[0:1, D : D + HD], in_=q_norm_w.unsqueeze(0))
        nc.sync.dma_start(out=zrow[0:1, D + HD : D + 2 * HD], in_=k_norm_w.unsqueeze(0))
        nc.sync.dma_start(out=zrow[0:1, 0:D], in_=ln1_w.unsqueeze(0))
        nc.sync.dma_start(out=wq_raw[:, :, 256:512], in_=wq_view[:, :, 256:512])
        load_x(1)
        nc.sync.dma_start(out=wk_raw[:], in_=Wk.rearrange("(p t) n -> p t n", t=4))
        nc.sync.dma_start(out=wv_raw[:], in_=Wv.rearrange("(p t) n -> p t n", t=4))
        load_cs(0)
        load_x(2)
        load_x(3)
        load_cs(1)
        load_x(4)
        load_x(5)
        load_cs(2)
        load_x(6)
        load_x(7)
        load_cs(3)
        load_x(8)
        load_x(9)
        load_x(10)
        load_x(11)
        load_x(12)
        load_x(13)
        load_x(14)
        load_x(15)

        wn_ps = psum_t.tile([P, 2, HD], F32, tag="tp")
        nc.tensor.matmul(
            out=wn_ps[:].rearrange("p a d -> p (a d)"), lhsT=ones[:], rhs=zrow[:, D : D + 2 * HD],
            start=True, stop=True,
        )
        lnw_ps = psum_c.tile([P, D], F32)
        nc.tensor.matmul(out=lnw_ps[:], lhsT=ones[:], rhs=zrow[:, 0:D], start=True, stop=True)
        wtab = const.tile([P, 2, 2, HD], BF16)
        tab = const.tile([P, TPP, 2, 2, HD], F32)

        def norm_weight_table():
            nc.vector.tensor_copy(out=wtab[:, :, 0, :], in_=wn_ps[:])
            nc.vector.tensor_copy(out=wtab[:, :, 1, :], in_=wn_ps[:])

        def negate_upper_sines():
            upper = wtab[:, :, 1, HALF:HD]
            nc.vector.tensor_scalar_mul(out=upper, in0=upper, scalar1=-1.0)

        def build_tables(i0, count, engine=nc.gpsimd):
            shape = [P, count, 2, 2 * HD]
            engine.tensor_tensor(
                out=tab[:, i0 : i0 + count, :, :, :].rearrange("p i w s d -> p i w (s d)"),
                in0=cs_raw[:, i0 : i0 + count, :, :]
                .rearrange("p i s d -> p i (s d)")
                .unsqueeze(2)
                .to_broadcast(shape),
                in1=wtab[:].rearrange("p w s d -> p w (s d)").unsqueeze(1).to_broadcast(shape),
                op=ALU.mult,
            )

        wg = const.tile([P, NOUT, 4], BF16, align_bytes=64)
        wc = const.tile([P, NOUT], U32, align_bytes=64)
        ws = const.tile([P, NOUT], U8, align_bytes=64)

        def interleave(copy, raw, c0, c1):
            copy(
                out=wg[:, c0:c1, :].rearrange("p (c i) t -> p c t i", i=4),
                in_=raw.rearrange("p t (c i) -> p c t i", i=4),
            )

        def quant_w(c):
            cols = slice(512 * c, 512 * (c + 1))
            nc.vector.quantize_mx(
                out=wc[:, cols].bitcast(FP8X4),
                scales=ws[:, cols],
                in_=wg[:, cols, :].rearrange("p n t -> p (n t)"),
            )

        r0s, hs_, tps, hgs, h_codes, banks, rs, obs, zs = {}, {}, {}, {}, {}, {}, {}, {}, {}

        def stats(n):
            pr, a = n // 2, n % 2
            if a == 0:
                r0s[pr] = small.tile([P, 2], F32, name="ss0"), small.tile([P, 2], F32, name="r0")
            sq = junk.tile([P, D], BF16)
            nc.scalar.activation(
                out=sq[:], in_=x_sb[pr][:, a, :], func=ACT.Square, accum_out=r0s[pr][0][:, a : a + 1]
            )

        def token_scale(pr):
            ss0, r0 = r0s[pr]
            nc.scalar.activation(
                out=r0[:], in_=ss0[:], func=ACT.Abs_reciprocal_sqrt, scale=1.0 / D, bias=eps[:, 0:1]
            )

        def norm(n):
            pr, a = n // 2, n % 2
            if a == 0:
                hs_[pr] = hpool.tile([P, 2, D], BF16, name="h")
            nc.vector.scalar_tensor_tensor(
                out=hs_[pr][:, a, :], in0=x_sb[pr][:, a, :],
                scalar=r0s[pr][1][:, a : a + 1], in1=lnw_ps[:],
                op0=ALU.mult, op1=ALU.mult,
            )

        def transp(pr):
            tp = psum_t.tile([P, 2, 2, P], F32, tag="tp")
            for a in range(2):
                words = hs_[pr][:, a, :].bitcast(F32)
                for u in range(2):
                    nc.tensor.transpose(out=tp[:, a, u, :], in_=words[:, u : D // 2 : 2], identity=ident[:])
            tps[pr] = tp

        def codes_place(pr):
            if pr < PAIR_CALLS:
                return pr, 1
            return pr - (pr - PAIR_CALLS) % 2, 2

        def evac(pr):
            first, count = codes_place(pr)
            if pr == first:
                hgs[first] = hgpool.tile([P, 2 * count, P, 4], BF16, align_bytes=64, name="hg%d" % count)
            a0 = 2 * (pr - first)
            nc.scalar.copy(
                out=hgs[first][:, a0 : a0 + 2, :, :].bitcast(F32),
                in_=tps[pr][:].rearrange("p a u r -> p a r u"),
            )

        def quant(first):
            count = codes_place(first)[1]
            hc = codes.tile([P, 2 * P * count], U32, align_bytes=64, name="hc%d" % count)
            hs = codes.tile([P, 2 * P * count], U8, align_bytes=64, name="hs%d" % count)
            nc.vector.quantize_mx(
                out=hc[:].bitcast(FP8X4), scales=hs[:], in_=hgs[first][:].rearrange("p a r t -> p (a r t)")
            )
            h_codes[first] = (hc, hs)

        def mx(n, parts=(0, 1)):
            first = codes_place(n // 2)[0]
            hc, hs = h_codes[first]
            a = n - 2 * first
            tok = slice(P * a, P * (a + 1))
            if 0 in parts:
                pa = psum_a.tile([P, 512], F32, name="pa")
                pb = psum_b.tile([P, 512], F32, name="pb")
                banks[n] = (pa, pb)
            for c in parts:
                cols = slice(512 * c, 512 * (c + 1))
                nc.tensor.matmul_mx(
                    out=banks[n][c][:],
                    lhsT=hc[:, tok].bitcast(FP8X4), lhsT_scale=hs[:, tok],
                    rhs=wc[:, cols].bitcast(FP8X4), rhs_scale=ws[:, cols],
                    start=True, stop=True,
                )

        def head(n, k):
            pa, pb = banks[n]
            return pa[:, HD * k : HD * (k + 1)] if k < NQ else pb[:, HD * (k - NQ) : HD * (k - NQ + 1)]

        Q_PART, K_PART, V_PART = (out_0, 0, NQ), (out_1, NQ, NQ + NK), (out_2, NQ + NK, NQ + NK + NV)

        def store(n, tiles=2, parts=(Q_PART, K_PART, V_PART), queue=nc.sync):
            b, g, ii = where(n)
            rows = slice(GRP * g + ii, GRP * g + ii + tiles)
            for dst, h0, h1 in parts:
                queue.dma_start(
                    out=dst[b].rearrange("h (p i) d -> p h i d", i=TPP)[:, :, rows, :],
                    in_=obs[n // 2][:, h0:h1, n % 2 : n % 2 + tiles, :],
                )

        def sq_heads(n):
            if n % 2 == 0:
                obs[n // 2] = obpool.tile([P, 8, 2, HD], F32, name="ob")
            ob = obs[n // 2]
            ss = small.tile([P, 6], F32)
            for k in range(NQ + NK):
                sq1 = junk.tile([P, HD], BF16)
                nc.scalar.activation(out=sq1[:], in_=head(n, k), func=ACT.Square, accum_out=ss[:, k : k + 1])
            nc.scalar.copy(
                out=ob[:, 6:8, n % 2, :], in_=banks[n][1][:, 256:512].rearrange("p (h d) -> p h d", h=2)
            )
            r = small.tile([P, 6], F32)
            nc.scalar.activation(
                out=r[:], in_=ss[:], func=ACT.Abs_reciprocal_sqrt, scale=1.0 / HD, bias=eps[:, 0:1]
            )
            rs[n] = r

        def rope(n, k0=0, k1=NQ + NK):
            b, g, ii = where(n)
            if n % 2 == 0 and k0 == 0:
                zs[n // 2] = zpool.tile([P, 2, NQ + NK, 2, HD], F32, name="z")
            z = zs[n // 2]
            for k in range(k0, k1):
                nc.vector.scalar_tensor_tensor(
                    out=z[:, :, k, n % 2, :], in0=tab[:, GRP * g + ii, 0 if k < NQ else 1, :, :],
                    scalar=rs[n][:, k : k + 1],
                    in1=head(n, k).unsqueeze(1).to_broadcast([P, 2, HD]),
                    op0=ALU.mult, op1=ALU.mult,
                )

        def add(n, tiles=1, engine=nc.gpsimd, h0=0, h1=NQ + NK):
            z, ob = zs[n // 2], obs[n // 2]
            a0, a1 = n % 2, n % 2 + tiles
            engine.tensor_tensor(
                out=ob[:, h0:h1, a0:a1, :].rearrange("p k a (s d) -> p k a s d", s=2),
                in0=z[:, 0, h0:h1, a0:a1, :].rearrange("p k a (s d) -> p k a s d", s=2),
                in1=z[:, 1, h0:h1, a0:a1, :].rearrange("p k a (s d) -> p k a s d", s=2)[:, :, :, ::-1, :],
                op=ALU.add,
            )

        def when(f, idx, limit, *rest):
            if 0 <= idx < limit:
                f(idx, *rest)

        PAIR_CALLS = n_pairs
        stats(0)
        stats(1)
        token_scale(0)
        stats(2)
        stats(3)
        token_scale(1)
        interleave(nc.vector.tensor_copy, wq_raw[:, :, 0:256], 0, 256)
        interleave(nc.vector.tensor_copy, wq_raw[:, :, 256:512], 256, 512)
        norm(0)
        norm(1)
        norm_weight_table()
        transp(0)
        interleave(nc.scalar.copy, wv_raw[:], 768, 1024)
        evac(0)
        stats(4)
        stats(5)
        token_scale(2)
        quant_w(0)
        interleave(nc.vector.tensor_copy, wk_raw[:], 512, 768)
        norm(2)
        quant(0)
        mx(0, (0,))
        quant_w(1)
        mx(0, (1,))
        mx(1)
        negate_upper_sines()
        for i in range(4):
            build_tables(i, 1)
        norm(3)
        transp(1)
        sq_heads(0)
        norm(4)
        norm(5)
        transp(2)
        stats(6)
        evac(1)
        sq_heads(1)
        rope(0)
        quant(1)
        mx(2)
        mx(3)
        stats(7)
        evac(2)
        token_scale(3)
        rope(1)
        quant(2)
        add(0, 2)
        store(0)
        norm(6)
        norm(7)
        transp(3)
        sq_heads(2)
        sq_heads(3)
        store(2, 2, (V_PART,))
        build_tables(4, 1)
        stats(8)
        stats(9)

        for n in range(2, n_tiles):
            when(mx, n + 2, n_tiles)
            if n % 2 == 0:
                when(evac, n // 2 + 2, n_pairs)
                when(token_scale, n // 2 + 3, n_pairs)
            when(sq_heads, n + 2, n_tiles)
            if n % 2 == 1 and n + 2 < n_tiles:
                store(n + 1, 2, (V_PART,), nc.sync if n < 19 else nc.scalar)
            rope(n)
            if n % 2 == 1:
                when(quant, (n + 3) // 2, n_pairs)
                if n < 28:
                    add(n - 1, 2)
                when(norm, n + 5, n_tiles)
                when(norm, n + 6, n_tiles)
                when(transp, (n + 5) // 2, n_pairs)
                when(build_tables, n // 2 + 4, TPP, 1)
                if n < 28:
                    store(n - 1, 2, (Q_PART, K_PART))
            if n in (28, 29):
                add(n)
                store(n, 1, (Q_PART, K_PART))
            when(stats, n + 8, n_tiles)
        add(30, 1, nc.vector)
        store(30, 1, (Q_PART, K_PART))
        add(31, 1, nc.vector, 0, NQ)
        store(31, 1, (Q_PART,))
        add(31, 1, nc.vector, NQ, NQ + NK)
        store(31, 1, (K_PART,))
